import numpy as np
import ml_dtypes


def mxq(x, axis, fmt="e4m3"):
    dtype, down = {"e4m3": (ml_dtypes.float8_e4m3fn, 7), "e5m2": (ml_dtypes.float8_e5m2, 14)}[fmt]
    v = np.moveaxis(np.asarray(x, np.float32).astype(ml_dtypes.bfloat16).astype(np.float64), axis, -1)
    blocks = v.reshape(v.shape[:-1] + (-1, 32))
    amax = np.abs(blocks).max(-1, keepdims=True)
    byte = np.maximum(np.where(amax > 0, np.frexp(amax)[1] - 1 + 127, 0) - down, 1)
    scale = np.exp2(byte - 127.0)
    codes = (blocks / scale).astype(np.float32).astype(dtype).astype(np.float64)
    return np.moveaxis((codes * scale).reshape(v.shape), -1, axis)


WIDE = False


def mx_kscale(k):
    if not WIDE:
        return np.ones(k)
    levels = np.array([10, -10, 5, -5, 0])
    a = np.random.permutation(np.resize(levels, k // 512 * 4)).reshape(k // 512, 4)
    idx = np.arange(k)
    return np.exp2(a[idx // 512, idx % 128 // 32])


BF16 = ml_dtypes.bfloat16


def bf(x):
    return np.asarray(x, np.float32).astype(BF16)


def f64(x):
    return np.asarray(x).astype(np.float64)


B, T, L, D, K = 4, 512, 256, 1024, 128
AG = 0.145 * np.sqrt(T)
EPS = 1e-5


def sigmoid(v):
    return 1.0 / (1.0 + np.exp(-v))


def layer_norm(x, g, b):
    m = x.mean(-1, keepdims=True)
    v = ((x - m) ** 2).mean(-1, keepdims=True)
    return (x - m) / np.sqrt(v + EPS) * g + b


def setup_inputs():
    s = mx_kscale(D)
    return {"agg": bf(np.random.standard_normal((B, K, D)) * AG * s),
            "M_old": bf(np.random.standard_normal((B, K, D))),
            "W_ih": bf(np.random.standard_normal((3 * D, D)) / (AG * np.sqrt(D)) / s),
            "W_hh": bf(np.random.standard_normal((3 * D, D)) / np.sqrt(D)),
            "b_ih": bf(np.random.standard_normal(3 * D) * 0.3),
            "b_hh": bf(np.random.standard_normal(3 * D) * 0.3),
            "g_mem": bf(1.0 + 0.1 * np.random.standard_normal(D)),
            "b_mem": bf(0.1 * np.random.standard_normal(D)),
            "Wk": bf(np.random.standard_normal((D, D)) / np.sqrt(D)),
            "Wv": bf(np.random.standard_normal((D, D)) / np.sqrt(D))}


def reference(agg, M_old, W_ih, W_hh, b_ih, b_hh, g_mem, b_mem, Wk, Wv):
    m = f64(M_old)
    gi = (mxq(f64(agg), 2, "e4m3") @ mxq(f64(W_ih), 1, "e4m3").T) + f64(b_ih)
    gh = (mxq(m, 2, "e4m3") @ mxq(f64(W_hh), 1, "e4m3").T) + f64(b_hh)
    gi_r, gi_z, gi_n = np.split(gi, 3, axis=-1)
    gh_r, gh_z, gh_n = np.split(gh, 3, axis=-1)
    r = sigmoid(gi_r + gh_r)
    z = sigmoid(gi_z + gh_z)
    n = np.tanh(gi_n + r * gh_n)
    h_new = (1.0 - z) * n + z * m
    m_new = layer_norm(h_new, f64(g_mem), f64(b_mem))
    mq = mxq(m_new, 2, "e4m3")
    kt = mq @ mxq(f64(Wk), 1, "e4m3").T
    v = mq @ mxq(f64(Wv), 1, "e4m3").T
    return kt, v

@@ -1,0 +1,411 @@
+from contextlib import ExitStack
+
+import concourse.masks as masks
+import concourse.mybir as mybir
+
+F32 = mybir.dt.float32
+BF16 = mybir.dt.bfloat16
+U32 = mybir.dt.uint32
+I32 = mybir.dt.int32
+U8 = mybir.dt.uint8
+FP8X4 = mybir.dt.float8_e4m3fn_x4
+ACT = mybir.ActivationFunctionType
+ALU = mybir.AluOpType
+
+P = 128
+D = 1024
+TOK = 512
+EPS = 1e-5
+FLOPS = 2 * TOK * D * 8 * D
+
+RAWB = 10
+GRPB = 5
+WCB = 9
+EVAC = "SSSSSSVS"
+HEAD_T = 4
+TS = (4, 4, 4, 3, 3, 3, 3, 0, 0)
+POOL_OPS = ()
+
+
+def tile_instrumentspecificslotmemory_pb_kernel(
+    tc, agg, M_old, W_ih, W_hh, b_ih, b_hh, g_mem, b_mem, Wk, Wv, out_0, out_1
+):
+    nc = tc.nc
+    with ExitStack() as ctx:
+        ctx.enter_context(tc.manual_schedule())
+        const = ctx.enter_context(tc.tile_pool(name="const", bufs=1))
+        rawp = ctx.enter_context(tc.tile_pool(name="rawp", bufs=RAWB))
+        grpp = ctx.enter_context(tc.tile_pool(name="grpp", bufs=GRPB))
+        wcp = ctx.enter_context(tc.tile_pool(name="wcp", bufs=WCB))
+        work = ctx.enter_context(tc.tile_pool(name="work", bufs=2))
+        lnp = ctx.enter_context(tc.tile_pool(name="lnp", bufs=4))
+        outp = ctx.enter_context(tc.tile_pool(name="outp", bufs=3))
+        psum = ctx.enter_context(tc.psum_pool(name="psum", bufs=8))
+
+        act_v = {
+            "agg": agg.flatten_outer_dims().rearrange("(t p) k -> p t k", p=P),
+            "mo": M_old.flatten_outer_dims().rearrange("(t p) k -> p t k", p=P),
+        }
+        w1_v = {
+            "ih": W_ih.rearrange("(a p e) k -> p a e k", p=P, e=2),
+            "hh": W_hh.rearrange("(a p e) k -> p a e k", p=P, e=2),
+        }
+        w2_v = [Wk.rearrange("(j p) k -> p j k", p=P), Wv.rearrange("(j p) k -> p j k", p=P)]
+        outs = [out_0.flatten_outer_dims(), out_1.flatten_outer_dims()]
+
+        stream = [(q, j) for j in range(8) for q in (0, 2, 1)] + [("w2", m, ci) for m in range(2) for ci in range(4)]
+        names = [("agg", 0), ("agg", 1), ("mo", 0), ("mo", 1)] + stream
+
+        raw = {}
+
+        def load():
+            if len(raw) < len(names):
+                nm = names[len(raw)]
+                t = rawp.tile([P, 2, D], BF16, name="raw", tag="raw")
+                if nm[0] == "w2":
+                    nc.sync.dma_start(out=t[:], in_=w2_v[nm[1]][:, 2 * nm[2] : 2 * nm[2] + 2, :])
+                elif nm[0] in ("agg", "mo"):
+                    nc.sync.dma_start(out=t[:], in_=act_v[nm[0]][:, 2 * nm[1] : 2 * nm[1] + 2, :])
+                else:
+                    q, j = nm
+                    for i, x in enumerate(("ih", "hh")):
+                        nc.sync.dma_start(out=t[:, i, :], in_=w1_v[x][:, 4 * q + j // 2, j % 2, :])
+                raw[nm] = t
+
+        ident = const.tile([P, P], F32, name="ident")
+        masks.make_identity(nc, ident[:])
+        braw = const.tile([P, 256], BF16, name="braw")
+        nc.vector.memset(braw[:].bitcast(I32), 0)
+        nc.scalar.dma_start(out=braw[0:12, :], in_=b_ih.rearrange("(a w) -> a w", w=256))
+        nc.scalar.dma_start(out=braw[12:24, :], in_=b_hh.rearrange("(a w) -> a w", w=256))
+        nc.scalar.dma_start(out=braw[24:28, :], in_=g_mem.rearrange("(a w) -> a w", w=256))
+        nc.scalar.dma_start(out=braw[28:32, :], in_=b_mem.rearrange("(a w) -> a w", w=256))
+        for i in range(RAWB):
+            load()
+        eps_t = const.tile([P, 1], F32, name="eps_t")
+        nc.vector.memset(eps_t[:], EPS)
+        warm = const.tile([P, 1], F32, name="warm")
+        nc.scalar.activation(out=warm[:], in_=eps_t[:], func=ACT.Sigmoid)
+
+        a_grp = {(x, g): const.tile([P, 4 * TOK], BF16, name="agrp_%s%d" % (x, g), align_bytes=64) for x in ("agg", "mo") for g in range(2)}
+        a_c = {x: const.tile([P, 2, TOK], U32, name="ac_" + x, align_bytes=64) for x in ("agg", "mo")}
+        a_s = {x: const.tile([P, 2, TOK], U8, name="as_" + x, align_bytes=64) for x in ("agg", "mo")}
+        w2c = const.tile([P, 2, 2, 2, TOK], U32, name="w2c", align_bytes=64)
+        w2s = const.tile([P, 2, 2, 2, TOK], U8, name="w2s", align_bytes=64)
+        hT = const.tile([P, 8, TOK], F32, name="hT")
+        m2c = const.tile([P, 2, TOK], U32, name="m2c", align_bytes=64)
+        m2s = const.tile([P, 2, TOK], U8, name="m2s", align_bytes=64)
+
+        banks = {}
+        grp = {}
+        wc = {}
+        ws = {}
+
+        def copy_on(eng):
+            return nc.scalar.copy if eng == "S" else nc.vector.tensor_copy
+
+        def transposes(nm):
+            words = raw[nm][:].bitcast(F32)
+            for g in range(2):
+                bank = psum.tile([P, 2, 256], F32, name="ps", tag="ps")
+                for u in range(2):
+                    for s in range(2):
+                        nc.tensor.transpose(bank[:, u, s * P : (s + 1) * P], words[:, s, (2 * g + u) * P : (2 * g + u + 1) * P], ident[:])
+                banks[(nm, g)] = bank
+            load()
+
+        def evacuate(nm, g, eng):
+            if nm[0] in ("agg", "mo"):
+                dest = a_grp[(nm[0], g)][:].bitcast(F32)[:, nm[1] * 512 : (nm[1] + 1) * 512]
+            else:
+                if nm not in grp:
+                    grp[nm] = grpp.tile([P, 2048], BF16, name="grp", tag="grp", align_bytes=64)
+                dest = grp[nm][:].bitcast(F32)[:, g * 512 : (g + 1) * 512]
+            copy_on(eng)(out=dest.rearrange("p (o u) -> p o u", u=2), in_=banks[(nm, g)][:].rearrange("p u o -> p o u"))
+
+        def quantise_act(x, g):
+            nc.vector.quantize_mx(out=a_c[x][:, g, :].bitcast(FP8X4), scales=a_s[x][:, g, :], in_=a_grp[(x, g)][:])
+
+        def quantise(nm):
+            if nm[0] == "w2":
+                m, ci = nm[1], nm[2]
+                h, cp = ci // 2, ci % 2
+                for g in range(2):
+                    nc.vector.quantize_mx(
+                        out=w2c[:, m, g, h, cp * 256 : (cp + 1) * 256].bitcast(FP8X4),
+                        scales=w2s[:, m, g, h, cp * 256 : (cp + 1) * 256],
+                        in_=grp[nm][:, g * 1024 : (g + 1) * 1024],
+                    )
+            else:
+                wc[nm] = wcp.tile([P, 512], U32, name="wc", tag="wc", align_bytes=64)
+                ws[nm] = wcp.tile([P, 512], U8, name="ws", tag="ws", align_bytes=64)
+                nc.vector.quantize_mx(out=wc[nm][:].bitcast(FP8X4), scales=ws[nm][:], in_=grp[nm][:])
+
+        acc = {}
+
+        def mx_group(key, j, q, xs):
+            bank = psum.tile([P, TOK], F32, name="ps", tag="ps")
+            n = 2 * len(xs)
+            i = 0
+            for x in xs:
+                a = ("agg", "mo")[x]
+                for g in range(2):
+                    cols = slice((2 * g + x) * P, (2 * g + x + 1) * P)
+                    nc.tensor.matmul_mx(
+                        out=bank[:],
+                        lhsT=wc[(q, j)][:, cols].bitcast(FP8X4),
+                        lhsT_scale=ws[(q, j)][:, cols],
+                        rhs=a_c[a][:, g, :].bitcast(FP8X4),
+                        rhs_scale=a_s[a][:, g, :],
+                        start=(i == 0),
+                        stop=(i == n - 1),
+                    )
+                    i += 1
+            acc[(key, j)] = bank
+
+        bf = const.tile([P, 64], F32, name="bf")
+        brz = const.tile([P, 16], F32, name="brz")
+
+        def biases():
+            bank = psum.tile([P, TOK], F32, name="ps", tag="ps")
+            nc.tensor.transpose(bank[:, 0:P], braw[:].bitcast(F32), ident[:])
+            bw = const.tile([P, 32], F32, name="bw")
+            nc.vector.tensor_copy(out=bw[:], in_=bank[:, 0:32])
+            nc.vector.tensor_copy(out=bf[:], in_=bw[:].bitcast(BF16))
+            nc.vector.tensor_tensor(out=brz[:], in0=bf[:, 0:16], in1=bf[:, 24:40], op=ALU.add)
+
+        tl = {}
+
+        def ew(name):
+            return nc.gpsimd if name in POOL_OPS else nc.vector
+
+        def sig_r(j):
+            tl[("r", j)] = work.tile([P, TOK], F32, name="r", tag="r")
+            nc.scalar.activation(out=tl[("r", j)][:], in_=acc[("r", j)][:], func=ACT.Sigmoid, bias=brz[:, j : j + 1], scale=1.0)
+
+        def sig_z(j):
+            tl[("z", j)] = work.tile([P, TOK], F32, name="z", tag="z")
+            nc.scalar.activation(out=tl[("z", j)][:], in_=acc[("z", j)][:], func=ACT.Sigmoid, bias=brz[:, 8 + j : 9 + j], scale=1.0)
+
+        def pre_n(j):
+            t = work.tile([P, TOK], F32, name="t", tag="t")
+            tl[("t", j)] = t
+            nc.vector.scalar_tensor_tensor(out=t[:], in0=acc[("gh", j)][:], scalar=bf[:, 40 + j : 41 + j], in1=tl[("r", j)][:], op0=ALU.add, op1=ALU.mult)
+            nc.vector.tensor_tensor(out=t[:], in0=t[:], in1=acc[("gi", j)][:], op=ALU.add)
+
+        def tanh_n(j):
+            tl[("n", j)] = work.tile([P, TOK], F32, name="n", tag="n")
+            nc.scalar.activation(out=tl[("n", j)][:], in_=tl[("t", j)][:], func=ACT.Tanh, bias=bf[:, 16 + j : 17 + j], scale=1.0)
+
+        def blend_sub(j):
+            d = work.tile([P, TOK], F32, name="d", tag="d")
+            tl[("d", j)] = d
+            m = a_grp[("mo", j // 4)][:].rearrange("p (k t) -> p k t", t=4)[:, :, j % 4]
+            ew("sub").tensor_tensor(out=d[:], in0=m, in1=tl[("n", j)][:], op=ALU.subtract)
+
+        def blend_rest(j):
+            d = tl[("d", j)]
+            ew("mul").tensor_tensor(out=d[:], in0=d[:], in1=tl[("z", j)][:], op=ALU.mult)
+            ew("add").tensor_tensor(out=hT[:, j, :], in0=d[:], in1=tl[("n", j)][:], op=ALU.add)
+
+        for x in ("agg", "mo"):
+            for th in range(2):
+                transposes((x, th))
+                evacuate((x, th), 0, "S")
+                evacuate((x, th), 1, "V")
+            if x == "agg":
+                biases()
+            quantise_act(x, 0)
+            quantise_act(x, 1)
+        for nm in stream[:HEAD_T]:
+            transposes(nm)
+            evacuate(nm, 0, "S")
+            evacuate(nm, 1, "V")
+            quantise(nm)
+
+        pos = HEAD_T
+        trip = []
+        for s in range(9):
+            j = s
+            bk = [(nm, g) for nm in trip for g in range(2)]
+
+            def ev(i):
+                if i < len(bk):
+                    evacuate(bk[i][0], bk[i][1], EVAC[i])
+
+            def qu(i):
+                if i < len(trip):
+                    quantise(trip[i])
+
+            ev(0)
+            ev(1)
+            if s > 0:
+                mx_group("z", j - 1, 1, (0, 1))
+            ev(2)
+            qu(0)
+            if s < 8:
+                mx_group("r", j, 0, (0, 1))
+            if s > 0:
+                sig_z(j - 1)
+            ev(3)
+            if s > 0:
+                blend_rest(j - 1)
+            if s < 8:
+                mx_group("gh", j, 2, (1,))
+                mx_group("gi", j, 2, (0,))
+                sig_r(j)
+            ev(4)
+            ev(5)
+            if s < 8:
+                pre_n(j)
+            qu(1)
+            qu(2)
+            for i in range(6, len(bk)):
+                ev(i)
+            for i in range(3, len(trip)):
+                qu(i)
+            trip = stream[pos : pos + TS[s]]
+            pos += TS[s]
+            for nm in trip:
+                transposes(nm)
+            if s < 8:
+                tanh_n(j)
+                blend_sub(j)
+        hb = {}
+        mv = {}
+        rstd = {}
+        nmr = {}
+        xn = {}
+        bb = {}
+        mn = {}
+
+        def fwd(tt):
+            for half in range(2):
+                bank = psum.tile([P, TOK], F32, name="ps", tag="ps")
+                for jj in range(4):
+                    nc.tensor.transpose(bank[:, jj * P : (jj + 1) * P], hT[:, 4 * half + jj, tt * P : (tt + 1) * P], ident[:])
+                hb[(tt, half)] = bank
+
+        def stats(tt):
+            st = lnp.tile([P, 2, 6], F32, name="st", tag="st")
+            for half in range(2):
+                nc.vector.bn_stats(out=st[:, half, :], in_=hb[(tt, half)][:])
+            mv[tt] = lnp.tile([P, 2], F32, name="mv", tag="mv")
+            nc.vector.bn_aggr(out=mv[tt][:], in_=st[:].rearrange("p a b -> p (a b)"))
+
+        def scale_of(tt):
+            sd = lnp.tile([P, 1], F32, name="sd", tag="sd")
+            nc.scalar.activation(out=sd[:], in_=mv[tt][:, 1:2], func=ACT.Sqrt, bias=eps_t[:, 0:1], scale=1.0)
+            rstd[tt] = lnp.tile([P, 1], F32, name="rstd", tag="rstd")
+            nc.vector.reciprocal(out=rstd[tt][:], in_=sd[:])
+            nmr[tt] = lnp.tile([P, 1], F32, name="nmr", tag="nmr")
+            nc.vector.scalar_tensor_tensor(out=nmr[tt][:], in0=mv[tt][:, 0:1], scalar=-1.0, in1=rstd[tt][:], op0=ALU.mult, op1=ALU.mult)
+
+        def norm(tt, engs):
+            xn[tt] = lnp.tile([P, D], F32, name="xn", tag="xn")
+            for half in range(2):
+                dst = xn[tt][:, half * 512 : (half + 1) * 512]
+                if engs[half] == "S":
+                    nc.scalar.activation(out=dst, in_=hb[(tt, half)][:], func=ACT.Identity, bias=nmr[tt][:, 0:1], scale=rstd[tt][:, 0:1])
+                else:
+                    nc.vector.tensor_scalar(out=dst, in0=hb[(tt, half)][:], scalar1=mv[tt][:, 0:1], scalar2=rstd[tt][:, 0:1], op0=ALU.subtract, op1=ALU.mult)
+
+        def back(tt):
+            for g in range(2):
+                bank = psum.tile([P, 4, P], F32, name="ps", tag="ps")
+                for t in range(4):
+                    nc.tensor.transpose(bank[:, t, :], xn[tt][:, (4 * g + t) * P : (4 * g + t + 1) * P], ident[:])
+                bb[(tt, g)] = bank
+
+        def affine(tt, g, engs):
+            if g == 0:
+                mn[tt] = lnp.tile([P, 8, P], BF16, name="mn", tag="mn")
+            for t in range(4):
+                j = 4 * g + t
+                if engs[t] == "S":
+                    nc.scalar.activation(out=mn[tt][:, j, :], in_=bb[(tt, g)][:, t, :], func=ACT.Identity, bias=bf[:, 56 + j : 57 + j], scale=bf[:, 48 + j : 49 + j])
+                else:
+                    nc.vector.tensor_scalar(out=mn[tt][:, j, :], in0=bb[(tt, g)][:, t, :], scalar1=bf[:, 48 + j : 49 + j], scalar2=bf[:, 56 + j : 57 + j], op0=ALU.mult, op1=ALU.add)
+
+        def regroup(tt, g):
+            g2 = lnp.tile([P, 4 * P], BF16, name="g2", tag="g2", align_bytes=64)
+            nc.vector.tensor_copy(out=g2[:].rearrange("p (k t) -> p k t", t=4), in_=mn[tt][:, 4 * g : 4 * g + 4, :].rearrange("p t k -> p k t"))
+            cols = slice(tt * P, (tt + 1) * P)
+            nc.vector.quantize_mx(out=m2c[:, g, cols].bitcast(FP8X4), scales=m2s[:, g, cols], in_=g2[:])
+
+        def project(tt, m, engs):
+            osb = outp.tile([P, D], F32, name="osb", tag="osb")
+            for h in range(2):
+                bank = psum.tile([P, TOK], F32, name="ps", tag="ps")
+                for g in range(2):
+                    nc.tensor.matmul_mx(
+                        out=bank[:],
+                        lhsT=m2c[:, g, tt * P : (tt + 1) * P].bitcast(FP8X4),
+                        lhsT_scale=m2s[:, g, tt * P : (tt + 1) * P],
+                        rhs=w2c[:, m, g, h, :].bitcast(FP8X4),
+                        rhs_scale=w2s[:, m, g, h, :],
+                        start=(g == 0),
+                        stop=(g == 1),
+                    )
+                copy_on(engs[h])(out=osb[:, h * 512 : (h + 1) * 512], in_=bank[:])
+            nc.sync.dma_start(out=outs[m][tt * P : (tt + 1) * P, :], in_=osb[:])
+
+        def prep(nm, engs):
+            evacuate(nm, 0, engs[0])
+            evacuate(nm, 1, engs[1])
+            quantise(nm)
+
+        nc.scalar.activation(out=warm[:], in_=eps_t[:], func=ACT.Sqrt)
+        w = stream[pos:]
+        transposes(w[0])
+        transposes(w[1])
+        prep(w[0], "SS")
+        fwd(0)
+        stats(0)
+        prep(w[1], "SS")
+        fwd(1)
+        scale_of(0)
+        stats(1)
+        norm(0, "SS")
+        scale_of(1)
+        transposes(w[2])
+        back(0)
+        norm(1, "SS")
+        fwd(2)
+        stats(2)
+        affine(0, 0, "SSSS")
+        affine(0, 1, "SSSS")
+        regroup(0, 0)
+        scale_of(2)
+        regroup(0, 1)
+        back(1)
+        prep(w[2], "SV")
+        transposes(w[3])
+        fwd(3)
+        norm(2, "SS")
+        stats(3)
+        project(0, 0, "SV")
+        affine(1, 0, "SSSS")
+        affine(1, 1, "SSSS")
+        scale_of(3)
+        regroup(1, 0)
+        regroup(1, 1)
+        prep(w[3], "SV")
+        back(2)
+        norm(3, "SS")
+        project(1, 0, "SV")
+        project(0, 1, "SV")
+        affine(2, 0, "SSSS")
+        affine(2, 1, "SSSS")
+        regroup(2, 0)
+        regroup(2, 1)
+        back(3)
+        project(1, 1, "SV")
+        project(2, 0, "SV")
+        affine(3, 0, "SSSS")
+        affine(3, 1, "VVVV")
+        regroup(3, 0)
+        regroup(3, 1)
+        project(2, 1, "SV")
+        project(3, 0, "SV")
+        project(3, 1, "SV")

@@ -21,9 +21,6 @@ FLOPS = 2 * TOK * D * 8 * D
 RAWB = 10
 GRPB = 5
 WCB = 9
-EVAC = "SSSSSSVS"
-HEAD_T = 4
-TS = (4, 4, 4, 3, 3, 3, 3, 0, 0)
 POOL_OPS = ()
 
 
@@ -40,7 +37,15 @@ def tile_instrumentspecificslotmemory_pb_kernel(
         work = ctx.enter_context(tc.tile_pool(name="work", bufs=2))
         lnp = ctx.enter_context(tc.tile_pool(name="lnp", bufs=4))
         outp = ctx.enter_context(tc.tile_pool(name="outp", bufs=3))
-        psum = ctx.enter_context(tc.psum_pool(name="psum", bufs=8))
+        psum = ctx.enter_context(tc.psum_pool(name="psum", bufs=1))
+
+        ring = [0]
+
+        def bank(shape, i=None):
+            if i is None:
+                i = ring[0] % 8
+                ring[0] += 1
+            return psum.tile(shape, F32, name="b%d" % i, tag="b%d" % i)
 
         act_v = {
             "agg": agg.flatten_outer_dims().rearrange("(t p) k -> p t k", p=P),
@@ -104,14 +109,14 @@ def tile_instrumentspecificslotmemory_pb_kernel(
         def copy_on(eng):
             return nc.scalar.copy if eng == "S" else nc.vector.tensor_copy
 
-        def transposes(nm):
+        def transposes(nm, b=None):
             words = raw[nm][:].bitcast(F32)
             for g in range(2):
-                bank = psum.tile([P, 2, 256], F32, name="ps", tag="ps")
+                bk = bank([P, 2, 256], None if b is None else b + g)
                 for u in range(2):
                     for s in range(2):
-                        nc.tensor.transpose(bank[:, u, s * P : (s + 1) * P], words[:, s, (2 * g + u) * P : (2 * g + u + 1) * P], ident[:])
-                banks[(nm, g)] = bank
+                        nc.tensor.transpose(bk[:, u, s * P : (s + 1) * P], words[:, s, (2 * g + u) * P : (2 * g + u + 1) * P], ident[:])
+                banks[(nm, g)] = bk
             load()
 
         def evacuate(nm, g, eng):
@@ -123,8 +128,9 @@ def tile_instrumentspecificslotmemory_pb_kernel(
                 dest = grp[nm][:].bitcast(F32)[:, g * 512 : (g + 1) * 512]
             copy_on(eng)(out=dest.rearrange("p (o u) -> p o u", u=2), in_=banks[(nm, g)][:].rearrange("p u o -> p o u"))
 
-        def quantise_act(x, g):
-            nc.vector.quantize_mx(out=a_c[x][:, g, :].bitcast(FP8X4), scales=a_s[x][:, g, :], in_=a_grp[(x, g)][:])
+        def quantise_act(x, g, th):
+            cols = slice(th * 256, (th + 1) * 256)
+            nc.vector.quantize_mx(out=a_c[x][:, g, cols].bitcast(FP8X4), scales=a_s[x][:, g, cols], in_=a_grp[(x, g)][:, th * 1024 : (th + 1) * 1024])
 
         def quantise(nm):
             if nm[0] == "w2":
@@ -143,8 +149,8 @@ def tile_instrumentspecificslotmemory_pb_kernel(
 
         acc = {}
 
-        def mx_group(key, j, q, xs):
-            bank = psum.tile([P, TOK], F32, name="ps", tag="ps")
+        def mx_group(key, j, q, xs, b):
+            bk = bank([P, TOK], b)
             n = 2 * len(xs)
             i = 0
             for x in xs:
@@ -152,7 +158,7 @@ def tile_instrumentspecificslotmemory_pb_kernel(
                 for g in range(2):
                     cols = slice((2 * g + x) * P, (2 * g + x + 1) * P)
                     nc.tensor.matmul_mx(
-                        out=bank[:],
+                        out=bk[:],
                         lhsT=wc[(q, j)][:, cols].bitcast(FP8X4),
                         lhsT_scale=ws[(q, j)][:, cols],
                         rhs=a_c[a][:, g, :].bitcast(FP8X4),
@@ -161,16 +167,16 @@ def tile_instrumentspecificslotmemory_pb_kernel(
                         stop=(i == n - 1),
                     )
                     i += 1
-            acc[(key, j)] = bank
+            acc[(key, j)] = bk
 
         bf = const.tile([P, 64], F32, name="bf")
         brz = const.tile([P, 16], F32, name="brz")
 
-        def biases():
-            bank = psum.tile([P, TOK], F32, name="ps", tag="ps")
-            nc.tensor.transpose(bank[:, 0:P], braw[:].bitcast(F32), ident[:])
+        def biases(b):
+            bk = bank([P, TOK], b)
+            nc.tensor.transpose(bk[:, 0:P], braw[:].bitcast(F32), ident[:])
             bw = const.tile([P, 32], F32, name="bw")
-            nc.vector.tensor_copy(out=bw[:], in_=bank[:, 0:32])
+            nc.vector.tensor_copy(out=bw[:], in_=bk[:, 0:32])
             nc.vector.tensor_copy(out=bf[:], in_=bw[:].bitcast(BF16))
             nc.vector.tensor_tensor(out=brz[:], in0=bf[:, 0:16], in1=bf[:, 24:40], op=ALU.add)
 
@@ -187,10 +193,13 @@ def tile_instrumentspecificslotmemory_pb_kernel(
             tl[("z", j)] = work.tile([P, TOK], F32, name="z", tag="z")
             nc.scalar.activation(out=tl[("z", j)][:], in_=acc[("z", j)][:], func=ACT.Sigmoid, bias=brz[:, 8 + j : 9 + j], scale=1.0)
 
-        def pre_n(j):
+        def pre_n1(j):
             t = work.tile([P, TOK], F32, name="t", tag="t")
             tl[("t", j)] = t
             nc.vector.scalar_tensor_tensor(out=t[:], in0=acc[("gh", j)][:], scalar=bf[:, 40 + j : 41 + j], in1=tl[("r", j)][:], op0=ALU.add, op1=ALU.mult)
+
+        def pre_n2(j):
+            t = tl[("t", j)]
             nc.vector.tensor_tensor(out=t[:], in0=t[:], in1=acc[("gi", j)][:], op=ALU.add)
 
         def tanh_n(j):
@@ -208,69 +217,6 @@ def tile_instrumentspecificslotmemory_pb_kernel(
             ew("mul").tensor_tensor(out=d[:], in0=d[:], in1=tl[("z", j)][:], op=ALU.mult)
             ew("add").tensor_tensor(out=hT[:, j, :], in0=d[:], in1=tl[("n", j)][:], op=ALU.add)
 
-        for x in ("agg", "mo"):
-            for th in range(2):
-                transposes((x, th))
-                evacuate((x, th), 0, "S")
-                evacuate((x, th), 1, "V")
-            if x == "agg":
-                biases()
-            quantise_act(x, 0)
-            quantise_act(x, 1)
-        for nm in stream[:HEAD_T]:
-            transposes(nm)
-            evacuate(nm, 0, "S")
-            evacuate(nm, 1, "V")
-            quantise(nm)
-
-        pos = HEAD_T
-        trip = []
-        for s in range(9):
-            j = s
-            bk = [(nm, g) for nm in trip for g in range(2)]
-
-            def ev(i):
-                if i < len(bk):
-                    evacuate(bk[i][0], bk[i][1], EVAC[i])
-
-            def qu(i):
-                if i < len(trip):
-                    quantise(trip[i])
-
-            ev(0)
-            ev(1)
-            if s > 0:
-                mx_group("z", j - 1, 1, (0, 1))
-            ev(2)
-            qu(0)
-            if s < 8:
-                mx_group("r", j, 0, (0, 1))
-            if s > 0:
-                sig_z(j - 1)
-            ev(3)
-            if s > 0:
-                blend_rest(j - 1)
-            if s < 8:
-                mx_group("gh", j, 2, (1,))
-                mx_group("gi", j, 2, (0,))
-                sig_r(j)
-            ev(4)
-            ev(5)
-            if s < 8:
-                pre_n(j)
-            qu(1)
-            qu(2)
-            for i in range(6, len(bk)):
-                ev(i)
-            for i in range(3, len(trip)):
-                qu(i)
-            trip = stream[pos : pos + TS[s]]
-            pos += TS[s]
-            for nm in trip:
-                transposes(nm)
-            if s < 8:
-                tanh_n(j)
-                blend_sub(j)
         hb = {}
         mv = {}
         rstd = {}
@@ -281,10 +227,10 @@ def tile_instrumentspecificslotmemory_pb_kernel(
 
         def fwd(tt):
             for half in range(2):
-                bank = psum.tile([P, TOK], F32, name="ps", tag="ps")
+                bk = bank([P, TOK])
                 for jj in range(4):
-                    nc.tensor.transpose(bank[:, jj * P : (jj + 1) * P], hT[:, 4 * half + jj, tt * P : (tt + 1) * P], ident[:])
-                hb[(tt, half)] = bank
+                    nc.tensor.transpose(bk[:, jj * P : (jj + 1) * P], hT[:, 4 * half + jj, tt * P : (tt + 1) * P], ident[:])
+                hb[(tt, half)] = bk
 
         def stats(tt):
             st = lnp.tile([P, 2, 6], F32, name="st", tag="st")
@@ -312,10 +258,10 @@ def tile_instrumentspecificslotmemory_pb_kernel(
 
         def back(tt):
             for g in range(2):
-                bank = psum.tile([P, 4, P], F32, name="ps", tag="ps")
+                bk = bank([P, 4, P])
                 for t in range(4):
-                    nc.tensor.transpose(bank[:, t, :], xn[tt][:, (4 * g + t) * P : (4 * g + t + 1) * P], ident[:])
-                bb[(tt, g)] = bank
+                    nc.tensor.transpose(bk[:, t, :], xn[tt][:, (4 * g + t) * P : (4 * g + t + 1) * P], ident[:])
+                bb[(tt, g)] = bk
 
         def affine(tt, g, engs):
             if g == 0:
@@ -336,10 +282,10 @@ def tile_instrumentspecificslotmemory_pb_kernel(
         def project(tt, m, engs):
             osb = outp.tile([P, D], F32, name="osb", tag="osb")
             for h in range(2):
-                bank = psum.tile([P, TOK], F32, name="ps", tag="ps")
+                bk = bank([P, TOK])
                 for g in range(2):
                     nc.tensor.matmul_mx(
-                        out=bank[:],
+                        out=bk[:],
                         lhsT=m2c[:, g, tt * P : (tt + 1) * P].bitcast(FP8X4),
                         lhsT_scale=m2s[:, g, tt * P : (tt + 1) * P],
                         rhs=w2c[:, m, g, h, :].bitcast(FP8X4),
@@ -347,7 +293,7 @@ def tile_instrumentspecificslotmemory_pb_kernel(
                         start=(g == 0),
                         stop=(g == 1),
                     )
-                copy_on(engs[h])(out=osb[:, h * 512 : (h + 1) * 512], in_=bank[:])
+                copy_on(engs[h])(out=osb[:, h * 512 : (h + 1) * 512], in_=bk[:])
             nc.sync.dma_start(out=outs[m][tt * P : (tt + 1) * P, :], in_=osb[:])
 
         def prep(nm, engs):
@@ -355,23 +301,76 @@ def tile_instrumentspecificslotmemory_pb_kernel(
             evacuate(nm, 1, engs[1])
             quantise(nm)
 
-        nc.scalar.activation(out=warm[:], in_=eps_t[:], func=ACT.Sqrt)
-        w = stream[pos:]
+        biases(7)
+        for i, (x, th) in enumerate((("agg", 0), ("agg", 1), ("mo", 0), ("mo", 1))):
+            transposes((x, th), (2 * i) % 8)
+            evacuate((x, th), 0, "S")
+            evacuate((x, th), 1, "V")
+            quantise_act(x, 0, th)
+            quantise_act(x, 1, th)
+        tb = [0]
+
+        def tr(nm):
+            transposes(nm, 2 * (tb[0] % 2))
+            tb[0] += 1
+
+        for nm in stream[:3]:
+            tr(nm)
+            evacuate(nm, 0, "S")
+            evacuate(nm, 1, "V")
+            quantise(nm)
+
+        c3 = None
+        for j in range(8):
+            c1, c2 = stream[3 * j + 3], stream[3 * j + 4]
+            mx_group("r", j, 0, (0, 1), 4)
+            mx_group("gh", j, 2, (1,), 5)
+            if j > 0:
+                blend_sub(j - 1)
+                blend_rest(j - 1)
+                evacuate(c3, 0, "S")
+                evacuate(c3, 1, "S")
+            sig_r(j)
+            if j > 0:
+                quantise(c3)
+            pre_n1(j)
+            tr(c1)
+            tr(c2)
+            evacuate(c1, 0, "S")
+            evacuate(c1, 1, "S")
+            evacuate(c2, 0, "S")
+            evacuate(c2, 1, "S")
+            mx_group("gi", j, 2, (0,), 6)
+            mx_group("z", j, 1, (0, 1), 7)
+            quantise(c1)
+            pre_n2(j)
+            quantise(c2)
+            c3 = stream[3 * j + 5]
+            tr(c3)
+            tanh_n(j)
+            sig_z(j)
+
+        w = stream[27:]
+        ring[0] = 2 * (tb[0] % 2)
         transposes(w[0])
-        transposes(w[1])
+        blend_sub(7)
+        blend_rest(7)
+        prep(c3, "SS")
+        nc.scalar.activation(out=warm[:], in_=eps_t[:], func=ACT.Sqrt)
         prep(w[0], "SS")
+        ring[0] = 4
         fwd(0)
-        stats(0)
-        prep(w[1], "SS")
         fwd(1)
+        stats(0)
         scale_of(0)
         stats(1)
         norm(0, "SS")
         scale_of(1)
-        transposes(w[2])
+        transposes(w[1])
         back(0)
         norm(1, "SS")
         fwd(2)
+        prep(w[1], "SV")
         stats(2)
         affine(0, 0, "SSSS")
         affine(0, 1, "SSSS")
@@ -379,10 +378,10 @@ def tile_instrumentspecificslotmemory_pb_kernel(
         scale_of(2)
         regroup(0, 1)
         back(1)
-        prep(w[2], "SV")
-        transposes(w[3])
+        transposes(w[2])
         fwd(3)
         norm(2, "SS")
+        prep(w[2], "SV")
         stats(3)
         project(0, 0, "SV")
         affine(1, 0, "SSSS")
@@ -390,16 +389,19 @@ def tile_instrumentspecificslotmemory_pb_kernel(
         scale_of(3)
         regroup(1, 0)
         regroup(1, 1)
+        transposes(w[3])
         prep(w[3], "SV")
         back(2)
         norm(3, "SS")
         project(1, 0, "SV")
-        project(0, 1, "SV")
+        transposes(w[4])
+        prep(w[4], "SV")
         affine(2, 0, "SSSS")
         affine(2, 1, "SSSS")
         regroup(2, 0)
         regroup(2, 1)
         back(3)
+        project(0, 1, "SV")
         project(1, 1, "SV")
         project(2, 0, "SV")
         affine(3, 0, "SSSS")

@@ -22,6 +22,22 @@ RAWB = 10
 GRPB = 5
 WCB = 9
 POOL_OPS = ()
+TAIL = (
+    ("tanh",), ("T", 5), ("T", 7), ("sigz",), ("Q", 1),
+    ("blend",), ("E", 5, "SS"), ("T", 4), ("E", 7, "SS"), ("E", 4, "VS"),
+    ("T", 6), ("F", 0), ("E", 6, "SS"), ("F", 1), ("Q", 7),
+    ("T", 3), ("T", 2), ("E", 3, "SS"), ("st", 0), ("st", 1),
+    ("sq", 0), ("F", 2), ("sq", 1), ("Q", 3), ("rc", 0),
+    ("E", 2, "SS"), ("nm", 0, "SS"), ("rc", 1), ("Q", 6), ("F", 3),
+    ("nm", 1, "SS"), ("st", 2), ("B", 0), ("sq", 2), ("st", 3),
+    ("rc", 2), ("af", 0, "SS"), ("nm", 2, "VS"), ("B", 1), ("B", 2),
+    ("sq", 3), ("af", 1, "SS"), ("rg", 0), ("af", 2, "SS"), ("Q", 5),
+    ("Q", 2), ("rg", 1), ("P", 0, 0), ("rc", 3), ("rg", 2),
+    ("P", 1, 0), ("P", 2, 0), ("oe", 0, 0, "SV"), ("nm", 3, "VS"), ("Q", 4),
+    ("B", 3), ("oe", 1, 0, "SS"), ("oe", 2, 0, "SS"), ("af", 3, "VV"), ("P", 2, 1),
+    ("P", 1, 1), ("oe", 2, 1, "SS"), ("rg", 3), ("oe", 1, 1, "SV"), ("P", 0, 1),
+    ("P", 3, 0), ("oe", 0, 1, "VS"), ("P", 3, 1), ("oe", 3, 0, "SS"), ("oe", 3, 1, "SV"),
+)
 
 
 def tile_instrumentspecificslotmemory_pb_kernel(
@@ -36,16 +52,22 @@ def tile_instrumentspecificslotmemory_pb_kernel(
         wcp = ctx.enter_context(tc.tile_pool(name="wcp", bufs=WCB))
         work = ctx.enter_context(tc.tile_pool(name="work", bufs=2))
         lnp = ctx.enter_context(tc.tile_pool(name="lnp", bufs=4))
-        outp = ctx.enter_context(tc.tile_pool(name="outp", bufs=3))
+        outp = ctx.enter_context(tc.tile_pool(name="outp", bufs=6))
         psum = ctx.enter_context(tc.psum_pool(name="psum", bufs=1))
 
-        ring = [0]
+        spare = [0, 1, 2, 3, 4, 5, 6]
+        taken = [0]
+        held = {}
 
-        def bank(shape, i=None):
+        def bank(key, shape, i=None):
             if i is None:
-                i = ring[0] % 8
-                ring[0] += 1
+                i = spare[taken[0]]
+                taken[0] += 1
+            held[key] = i
             return psum.tile(shape, F32, name="b%d" % i, tag="b%d" % i)
+
+        def give(key):
+            spare.extend([held[key]])
 
         act_v = {
             "agg": agg.flatten_outer_dims().rearrange("(t p) k -> p t k", p=P),
@@ -112,7 +134,7 @@ def tile_instrumentspecificslotmemory_pb_kernel(
         def transposes(nm, b=None):
             words = raw[nm][:].bitcast(F32)
             for g in range(2):
-                bk = bank([P, 2, 256], None if b is None else b + g)
+                bk = bank((nm, g), [P, 2, 256], None if b is None else b + g)
                 for u in range(2):
                     for s in range(2):
                         nc.tensor.transpose(bk[:, u, s * P : (s + 1) * P], words[:, s, (2 * g + u) * P : (2 * g + u + 1) * P], ident[:])
@@ -127,6 +149,7 @@ def tile_instrumentspecificslotmemory_pb_kernel(
                     grp[nm] = grpp.tile([P, 2048], BF16, name="grp", tag="grp", align_bytes=64)
                 dest = grp[nm][:].bitcast(F32)[:, g * 512 : (g + 1) * 512]
             copy_on(eng)(out=dest.rearrange("p (o u) -> p o u", u=2), in_=banks[(nm, g)][:].rearrange("p u o -> p o u"))
+            give((nm, g))
 
         def quantise_act(x, g, th):
             cols = slice(th * 256, (th + 1) * 256)
@@ -150,7 +173,7 @@ def tile_instrumentspecificslotmemory_pb_kernel(
         acc = {}
 
         def mx_group(key, j, q, xs, b):
-            bk = bank([P, TOK], b)
+            bk = bank((key, j), [P, TOK], b)
             n = 2 * len(xs)
             i = 0
             for x in xs:
@@ -173,7 +196,7 @@ def tile_instrumentspecificslotmemory_pb_kernel(
         brz = const.tile([P, 16], F32, name="brz")
 
         def biases(b):
-            bk = bank([P, TOK], b)
+            bk = bank("bias", [P, TOK], b)
             nc.tensor.transpose(bk[:, 0:P], braw[:].bitcast(F32), ident[:])
             bw = const.tile([P, 32], F32, name="bw")
             nc.vector.tensor_copy(out=bw[:], in_=bk[:, 0:32])
@@ -227,7 +250,7 @@ def tile_instrumentspecificslotmemory_pb_kernel(
 
         def fwd(tt):
             for half in range(2):
-                bk = bank([P, TOK])
+                bk = bank(("F", tt, half), [P, TOK])
                 for jj in range(4):
                     nc.tensor.transpose(bk[:, jj * P : (jj + 1) * P], hT[:, 4 * half + jj, tt * P : (tt + 1) * P], ident[:])
                 hb[(tt, half)] = bk
@@ -239,9 +262,14 @@ def tile_instrumentspecificslotmemory_pb_kernel(
             mv[tt] = lnp.tile([P, 2], F32, name="mv", tag="mv")
             nc.vector.bn_aggr(out=mv[tt][:], in_=st[:].rearrange("p a b -> p (a b)"))
 
+        sdv = {}
+
+        def root(tt):
+            sdv[tt] = lnp.tile([P, 1], F32, name="sd", tag="sd")
+            nc.scalar.activation(out=sdv[tt][:], in_=mv[tt][:, 1:2], func=ACT.Sqrt, bias=eps_t[:, 0:1], scale=1.0)
+
         def scale_of(tt):
-            sd = lnp.tile([P, 1], F32, name="sd", tag="sd")
-            nc.scalar.activation(out=sd[:], in_=mv[tt][:, 1:2], func=ACT.Sqrt, bias=eps_t[:, 0:1], scale=1.0)
+            sd = sdv[tt]
             rstd[tt] = lnp.tile([P, 1], F32, name="rstd", tag="rstd")
             nc.vector.reciprocal(out=rstd[tt][:], in_=sd[:])
             nmr[tt] = lnp.tile([P, 1], F32, name="nmr", tag="nmr")
@@ -255,10 +283,11 @@ def tile_instrumentspecificslotmemory_pb_kernel(
                     nc.scalar.activation(out=dst, in_=hb[(tt, half)][:], func=ACT.Identity, bias=nmr[tt][:, 0:1], scale=rstd[tt][:, 0:1])
                 else:
                     nc.vector.tensor_scalar(out=dst, in0=hb[(tt, half)][:], scalar1=mv[tt][:, 0:1], scalar2=rstd[tt][:, 0:1], op0=ALU.subtract, op1=ALU.mult)
+                give(("F", tt, half))
 
         def back(tt):
             for g in range(2):
-                bk = bank([P, 4, P])
+                bk = bank(("B", tt, g), [P, 4, P])
                 for t in range(4):
                     nc.tensor.transpose(bk[:, t, :], xn[tt][:, (4 * g + t) * P : (4 * g + t + 1) * P], ident[:])
                 bb[(tt, g)] = bk
@@ -272,6 +301,7 @@ def tile_instrumentspecificslotmemory_pb_kernel(
                     nc.scalar.activation(out=mn[tt][:, j, :], in_=bb[(tt, g)][:, t, :], func=ACT.Identity, bias=bf[:, 56 + j : 57 + j], scale=bf[:, 48 + j : 49 + j])
                 else:
                     nc.vector.tensor_scalar(out=mn[tt][:, j, :], in0=bb[(tt, g)][:, t, :], scalar1=bf[:, 48 + j : 49 + j], scalar2=bf[:, 56 + j : 57 + j], op0=ALU.mult, op1=ALU.add)
+            give(("B", tt, g))
 
         def regroup(tt, g):
             g2 = lnp.tile([P, 4 * P], BF16, name="g2", tag="g2", align_bytes=64)
@@ -279,10 +309,11 @@ def tile_instrumentspecificslotmemory_pb_kernel(
             cols = slice(tt * P, (tt + 1) * P)
             nc.vector.quantize_mx(out=m2c[:, g, cols].bitcast(FP8X4), scales=m2s[:, g, cols], in_=g2[:])
 
-        def project(tt, m, engs):
-            osb = outp.tile([P, D], F32, name="osb", tag="osb")
+        pb = {}
+
+        def project(tt, m):
             for h in range(2):
-                bk = bank([P, TOK])
+                bk = bank(("P", tt, m, h), [P, TOK])
                 for g in range(2):
                     nc.tensor.matmul_mx(
                         out=bk[:],
@@ -293,13 +324,14 @@ def tile_instrumentspecificslotmemory_pb_kernel(
                         start=(g == 0),
                         stop=(g == 1),
                     )
-                copy_on(engs[h])(out=osb[:, h * 512 : (h + 1) * 512], in_=bk[:])
-            nc.sync.dma_start(out=outs[m][tt * P : (tt + 1) * P, :], in_=osb[:])
+                pb[(tt, m, h)] = bk
 
-        def prep(nm, engs):
-            evacuate(nm, 0, engs[0])
-            evacuate(nm, 1, engs[1])
-            quantise(nm)
+        def results(tt, m, engs):
+            for h in range(2):
+                osb = outp.tile([P, TOK], F32, name="osb", tag="osb")
+                copy_on(engs[h])(out=osb[:], in_=pb[(tt, m, h)][:])
+                give(("P", tt, m, h))
+                nc.sync.dma_start(out=outs[m][tt * P : (tt + 1) * P, h * TOK : (h + 1) * TOK], in_=osb[:])
 
         biases(7)
         for i, (x, th) in enumerate((("agg", 0), ("agg", 1), ("mo", 0), ("mo", 1))):
@@ -344,70 +376,53 @@ def tile_instrumentspecificslotmemory_pb_kernel(
             mx_group("z", j, 1, (0, 1), 7)
             quantise(c1)
             pre_n2(j)
-            quantise(c2)
-            c3 = stream[3 * j + 5]
-            tr(c3)
-            tanh_n(j)
-            sig_z(j)
+            if j < 7:
+                quantise(c2)
+                c3 = stream[3 * j + 5]
+                tr(c3)
+                tanh_n(j)
+                sig_z(j)
 
-        w = stream[27:]
-        ring[0] = 2 * (tb[0] % 2)
-        transposes(w[0])
-        blend_sub(7)
-        blend_rest(7)
-        prep(c3, "SS")
-        nc.scalar.activation(out=warm[:], in_=eps_t[:], func=ACT.Sqrt)
-        prep(w[0], "SS")
-        ring[0] = 4
-        fwd(0)
-        fwd(1)
-        stats(0)
-        scale_of(0)
-        stats(1)
-        norm(0, "SS")
-        scale_of(1)
-        transposes(w[1])
-        back(0)
-        norm(1, "SS")
-        fwd(2)
-        prep(w[1], "SV")
-        stats(2)
-        affine(0, 0, "SSSS")
-        affine(0, 1, "SSSS")
-        regroup(0, 0)
-        scale_of(2)
-        regroup(0, 1)
-        back(1)
-        transposes(w[2])
-        fwd(3)
-        norm(2, "SS")
-        prep(w[2], "SV")
-        stats(3)
-        project(0, 0, "SV")
-        affine(1, 0, "SSSS")
-        affine(1, 1, "SSSS")
-        scale_of(3)
-        regroup(1, 0)
-        regroup(1, 1)
-        transposes(w[3])
-        prep(w[3], "SV")
-        back(2)
-        norm(3, "SS")
-        project(1, 0, "SV")
-        transposes(w[4])
-        prep(w[4], "SV")
-        affine(2, 0, "SSSS")
-        affine(2, 1, "SSSS")
-        regroup(2, 0)
-        regroup(2, 1)
-        back(3)
-        project(0, 1, "SV")
-        project(1, 1, "SV")
-        project(2, 0, "SV")
-        affine(3, 0, "SSSS")
-        affine(3, 1, "VVVV")
-        regroup(3, 0)
-        regroup(3, 1)
-        project(2, 1, "SV")
-        project(3, 0, "SV")
-        project(3, 1, "SV")
+        w = stream[24:]
+        taken[0] = len(spare)
+        spare.extend([0, 1, 2, 3, 4, 5, 6])
+        for op in TAIL:
+            k = op[0]
+            if k == "tanh":
+                tanh_n(7)
+            elif k == "sigz":
+                sig_z(7)
+                give(("z", 7))
+                nc.scalar.activation(out=warm[:], in_=eps_t[:], func=ACT.Sqrt)
+            elif k == "blend":
+                blend_sub(7)
+                blend_rest(7)
+            elif k == "T":
+                transposes(w[op[1]])
+            elif k == "E":
+                evacuate(w[op[1]], 0, op[2][0])
+                evacuate(w[op[1]], 1, op[2][1])
+            elif k == "Q":
+                quantise(w[op[1]])
+            elif k == "F":
+                fwd(op[1])
+            elif k == "st":
+                stats(op[1])
+            elif k == "sq":
+                root(op[1])
+            elif k == "rc":
+                scale_of(op[1])
+            elif k == "nm":
+                norm(op[1], op[2])
+            elif k == "B":
+                back(op[1])
+            elif k == "af":
+                affine(op[1], 0, op[2][0] * 4)
+                affine(op[1], 1, op[2][1] * 4)
+            elif k == "rg":
+                regroup(op[1], 0)
+                regroup(op[1], 1)
+            elif k == "P":
+                project(op[1], op[2])
+            else:
+                results(op[1], op[2], op[3])

@@ -23,20 +23,20 @@ GRPB = 5
 WCB = 9
 POOL_OPS = ()
 TAIL = (
-    ("tanh",), ("T", 5), ("T", 7), ("sigz",), ("Q", 1),
-    ("blend",), ("E", 5, "SS"), ("T", 4), ("E", 7, "SS"), ("E", 4, "VS"),
-    ("T", 6), ("F", 0), ("E", 6, "SS"), ("F", 1), ("Q", 7),
-    ("T", 3), ("T", 2), ("E", 3, "SS"), ("st", 0), ("st", 1),
-    ("sq", 0), ("F", 2), ("sq", 1), ("Q", 3), ("rc", 0),
-    ("E", 2, "SS"), ("nm", 0, "SS"), ("rc", 1), ("Q", 6), ("F", 3),
-    ("nm", 1, "SS"), ("st", 2), ("B", 0), ("sq", 2), ("st", 3),
-    ("rc", 2), ("af", 0, "SS"), ("nm", 2, "VS"), ("B", 1), ("B", 2),
-    ("sq", 3), ("af", 1, "SS"), ("rg", 0), ("af", 2, "SS"), ("Q", 5),
-    ("Q", 2), ("rg", 1), ("P", 0, 0), ("rc", 3), ("rg", 2),
-    ("P", 1, 0), ("P", 2, 0), ("oe", 0, 0, "SV"), ("nm", 3, "VS"), ("Q", 4),
-    ("B", 3), ("oe", 1, 0, "SS"), ("oe", 2, 0, "SS"), ("af", 3, "VV"), ("P", 2, 1),
-    ("P", 1, 1), ("oe", 2, 1, "SS"), ("rg", 3), ("oe", 1, 1, "SV"), ("P", 0, 1),
-    ("P", 3, 0), ("oe", 0, 1, "VS"), ("P", 3, 1), ("oe", 3, 0, "SS"), ("oe", 3, 1, "SV"),
+    ("T", 2), ("tanh",), ("T", 6), ("Q", 1), ("sigz",),
+    ("blend",), ("T", 7), ("E", 2, "SS"), ("T", 3), ("E", 7, "SS"),
+    ("E", 3, "VS"), ("T", 5), ("F", 0), ("Q", 2), ("st", 0),
+    ("F", 1), ("E", 6, "SS"), ("F", 2), ("sq", 0), ("st", 1),
+    ("st", 2), ("E", 5, "SS"), ("Q", 3), ("sq", 1), ("nm", 0, "SS"),
+    ("sq", 2), ("T", 4), ("nm", 1, "SS"), ("B", 0), ("af", 0, "SS"),
+    ("F", 3), ("nm", 2, "SS"), ("E", 4, "VS"), ("st", 3), ("rg", 0),
+    ("B", 1), ("af", 1, "VV"), ("B", 2), ("P", 0, 0), ("rg", 1),
+    ("P", 1, 0), ("sq", 3), ("af", 2, "SS"), ("nm", 3, "SS"), ("rg", 2),
+    ("Q", 5), ("oe", 0, 0, "SS"), ("oe", 1, 0, "SS"), ("P", 2, 0), ("B", 3),
+    ("Q", 4), ("oe", 2, 0, "SS"), ("Q", 7), ("Q", 6), ("P", 2, 1),
+    ("af", 3, "VV"), ("oe", 2, 1, "SS"), ("P", 1, 1), ("rg", 3), ("oe", 1, 1, "SS"),
+    ("P", 0, 1), ("P", 3, 0), ("oe", 0, 1, "VV"), ("P", 3, 1), ("oe", 3, 0, "SV"),
+    ("oe", 3, 1, "SV"),
 )
 
 
@@ -111,6 +111,8 @@ def tile_instrumentspecificslotmemory_pb_kernel(
             load()
         eps_t = const.tile([P, 1], F32, name="eps_t")
         nc.vector.memset(eps_t[:], EPS)
+        mhalf = const.tile([P, 1], F32, name="mhalf")
+        nc.vector.memset(mhalf[:], -0.5)
         warm = const.tile([P, 1], F32, name="warm")
         nc.scalar.activation(out=warm[:], in_=eps_t[:], func=ACT.Sigmoid)
 
@@ -242,6 +244,7 @@ def tile_instrumentspecificslotmemory_pb_kernel(
 
         hb = {}
         mv = {}
+        ve = {}
         rstd = {}
         nmr = {}
         xn = {}
@@ -261,19 +264,14 @@ def tile_instrumentspecificslotmemory_pb_kernel(
                 nc.vector.bn_stats(out=st[:, half, :], in_=hb[(tt, half)][:])
             mv[tt] = lnp.tile([P, 2], F32, name="mv", tag="mv")
             nc.vector.bn_aggr(out=mv[tt][:], in_=st[:].rearrange("p a b -> p (a b)"))
-
-        sdv = {}
+            ve[tt] = lnp.tile([P, 1], F32, name="ve", tag="ve")
+            nc.vector.tensor_scalar(out=ve[tt][:], in0=mv[tt][:, 1:2], scalar1=EPS, scalar2=None, op0=ALU.add)
 
         def root(tt):
-            sdv[tt] = lnp.tile([P, 1], F32, name="sd", tag="sd")
-            nc.scalar.activation(out=sdv[tt][:], in_=mv[tt][:, 1:2], func=ACT.Sqrt, bias=eps_t[:, 0:1], scale=1.0)
-
-        def scale_of(tt):
-            sd = sdv[tt]
             rstd[tt] = lnp.tile([P, 1], F32, name="rstd", tag="rstd")
-            nc.vector.reciprocal(out=rstd[tt][:], in_=sd[:])
+            nc.gpsimd.tensor_tensor(out=rstd[tt][:], in0=ve[tt][:], in1=mhalf[:], op=ALU.pow)
             nmr[tt] = lnp.tile([P, 1], F32, name="nmr", tag="nmr")
-            nc.vector.scalar_tensor_tensor(out=nmr[tt][:], in0=mv[tt][:, 0:1], scalar=-1.0, in1=rstd[tt][:], op0=ALU.mult, op1=ALU.mult)
+            nc.gpsimd.tensor_scalar(out=nmr[tt][:], in0=mv[tt][:, 0:1], scalar1=rstd[tt][:, 0:1], scalar2=-1.0, op0=ALU.mult, op1=ALU.mult)
 
         def norm(tt, engs):
             xn[tt] = lnp.tile([P, D], F32, name="xn", tag="xn")
@@ -393,7 +391,6 @@ def tile_instrumentspecificslotmemory_pb_kernel(
             elif k == "sigz":
                 sig_z(7)
                 give(("z", 7))
-                nc.scalar.activation(out=warm[:], in_=eps_t[:], func=ACT.Sqrt)
             elif k == "blend":
                 blend_sub(7)
                 blend_rest(7)
@@ -410,8 +407,6 @@ def tile_instrumentspecificslotmemory_pb_kernel(
                 stats(op[1])
             elif k == "sq":
                 root(op[1])
-            elif k == "rc":
-                scale_of(op[1])
             elif k == "nm":
                 norm(op[1], op[2])
             elif k == "B":

@@ -21,6 +21,8 @@ FLOPS = 2 * TOK * D * 8 * D
 RAWB = 10
 GRPB = 5
 WCB = 9
+WARM0 = 0
+WARM1 = 0
 POOL_OPS = ()
 TAIL = (
     ("T", 2), ("tanh",), ("T", 6), ("Q", 1), ("sigz",),
@@ -107,6 +109,8 @@ def tile_instrumentspecificslotmemory_pb_kernel(
         nc.scalar.dma_start(out=braw[12:24, :], in_=b_hh.rearrange("(a w) -> a w", w=256))
         nc.scalar.dma_start(out=braw[24:28, :], in_=g_mem.rearrange("(a w) -> a w", w=256))
         nc.scalar.dma_start(out=braw[28:32, :], in_=b_mem.rearrange("(a w) -> a w", w=256))
+        zt = const.tile([P, TOK], BF16, name="zt")
+        nc.vector.memset(zt[:].bitcast(I32), 0)
         for i in range(RAWB):
             load()
         eps_t = const.tile([P, 1], F32, name="eps_t")
@@ -331,14 +335,20 @@ def tile_instrumentspecificslotmemory_pb_kernel(
                 give(("P", tt, m, h))
                 nc.sync.dma_start(out=outs[m][tt * P : (tt + 1) * P, h * TOK : (h + 1) * TOK], in_=osb[:])
 
-        biases(7)
+        def idle_work(n):
+            for i in range(n):
+                bk = bank("idle", [P, TOK], 6)
+                nc.tensor.matmul(out=bk[:], lhsT=zt[:, 0:P], rhs=zt[:], start=True, stop=True)
+
+        idle_work(WARM0)
         for i, (x, th) in enumerate((("agg", 0), ("agg", 1), ("mo", 0), ("mo", 1))):
-            transposes((x, th), (2 * i) % 8)
+            transposes((x, th), (2 * i) % 6)
+            idle_work(WARM1)
             evacuate((x, th), 0, "S")
             evacuate((x, th), 1, "V")
             quantise_act(x, 0, th)
             quantise_act(x, 1, th)
-        tb = [0]
+        tb = [1]
 
         def tr(nm):
             transposes(nm, 2 * (tb[0] % 2))
@@ -346,6 +356,9 @@ def tile_instrumentspecificslotmemory_pb_kernel(
 
         for nm in stream[:3]:
             tr(nm)
+            idle_work(WARM1)
+            if nm == stream[0]:
+                biases(7)
             evacuate(nm, 0, "S")
             evacuate(nm, 1, "V")
             quantise(nm)

@@ -21,24 +21,25 @@ FLOPS = 2 * TOK * D * 8 * D
 RAWB = 10
 GRPB = 5
 WCB = 9
-WARM0 = 0
-WARM1 = 0
+WARM0 = 6
+WARM1 = 1
 POOL_OPS = ()
 TAIL = (
-    ("T", 2), ("tanh",), ("T", 6), ("Q", 1), ("sigz",),
-    ("blend",), ("T", 7), ("E", 2, "SS"), ("T", 3), ("E", 7, "SS"),
-    ("E", 3, "VS"), ("T", 5), ("F", 0), ("Q", 2), ("st", 0),
-    ("F", 1), ("E", 6, "SS"), ("F", 2), ("sq", 0), ("st", 1),
-    ("st", 2), ("E", 5, "SS"), ("Q", 3), ("sq", 1), ("nm", 0, "SS"),
-    ("sq", 2), ("T", 4), ("nm", 1, "SS"), ("B", 0), ("af", 0, "SS"),
-    ("F", 3), ("nm", 2, "SS"), ("E", 4, "VS"), ("st", 3), ("rg", 0),
-    ("B", 1), ("af", 1, "VV"), ("B", 2), ("P", 0, 0), ("rg", 1),
-    ("P", 1, 0), ("sq", 3), ("af", 2, "SS"), ("nm", 3, "SS"), ("rg", 2),
-    ("Q", 5), ("oe", 0, 0, "SS"), ("oe", 1, 0, "SS"), ("P", 2, 0), ("B", 3),
-    ("Q", 4), ("oe", 2, 0, "SS"), ("Q", 7), ("Q", 6), ("P", 2, 1),
-    ("af", 3, "VV"), ("oe", 2, 1, "SS"), ("P", 1, 1), ("rg", 3), ("oe", 1, 1, "SS"),
-    ("P", 0, 1), ("P", 3, 0), ("oe", 0, 1, "VV"), ("P", 3, 1), ("oe", 3, 0, "SV"),
-    ("oe", 3, 1, "SV"),
+    ("Q", 1), ("D", 2), ("tanh",), ("T", 2), ("sigz",),
+    ("E", 2, "SS"), ("T", 6), ("D", 1), ("E", 6, "SS"), ("blend",),
+    ("Q", 2), ("T", 7), ("Q", 6), ("E", 7, "SS"), ("F", 0),
+    ("T", 3), ("F", 1), ("D", 2), ("st", 0), ("sq", 0),
+    ("F", 2), ("st", 1), ("E", 3, "SS"), ("nm", 0, "SS"), ("sq", 1),
+    ("st", 2), ("T", 5), ("Q", 7), ("Q", 3), ("D", 1),
+    ("sq", 2), ("F", 3), ("nm", 1, "SS"), ("nm", 2, "SS"), ("D", 2),
+    ("st", 3), ("T", 4), ("sq", 3), ("E", 5, "SV"), ("B", 1),
+    ("D", 1), ("B", 0), ("af", 1, "SV"), ("nm", 3, "SV"), ("D", 2),
+    ("rg", 1), ("B", 3), ("af", 0, "SS"), ("E", 4, "VS"), ("B", 2),
+    ("P", 1, 0), ("rg", 0), ("Q", 5), ("P", 0, 0), ("Q", 4),
+    ("af", 2, "SV"), ("oe", 1, 0, "SS"), ("rg", 2), ("af", 3, "VV"), ("rg", 3),
+    ("oe", 0, 0, "SS"), ("P", 0, 1), ("P", 1, 1), ("oe", 0, 1, "SS"), ("oe", 1, 1, "SS"),
+    ("P", 2, 1), ("P", 2, 0), ("oe", 2, 1, "SS"), ("P", 3, 1), ("P", 3, 0),
+    ("oe", 2, 0, "VV"), ("oe", 3, 1, "VS"), ("oe", 3, 0, "SS"),
 )
 
 
@@ -110,7 +111,7 @@ def tile_instrumentspecificslotmemory_pb_kernel(
         nc.scalar.dma_start(out=braw[24:28, :], in_=g_mem.rearrange("(a w) -> a w", w=256))
         nc.scalar.dma_start(out=braw[28:32, :], in_=b_mem.rearrange("(a w) -> a w", w=256))
         zt = const.tile([P, TOK], BF16, name="zt")
-        nc.vector.memset(zt[:].bitcast(I32), 0)
+        nc.vector.memset(zt[:], 1.0)
         for i in range(RAWB):
             load()
         eps_t = const.tile([P, 1], F32, name="eps_t")
@@ -335,9 +336,9 @@ def tile_instrumentspecificslotmemory_pb_kernel(
                 give(("P", tt, m, h))
                 nc.sync.dma_start(out=outs[m][tt * P : (tt + 1) * P, h * TOK : (h + 1) * TOK], in_=osb[:])
 
-        def idle_work(n):
+        def idle_work(n, b=6):
             for i in range(n):
-                bk = bank("idle", [P, TOK], 6)
+                bk = bank("idle", [P, TOK], b)
                 nc.tensor.matmul(out=bk[:], lhsT=zt[:, 0:P], rhs=zt[:], start=True, stop=True)
 
         idle_work(WARM0)
@@ -407,6 +408,8 @@ def tile_instrumentspecificslotmemory_pb_kernel(
             elif k == "blend":
                 blend_sub(7)
                 blend_rest(7)
+            elif k == "D":
+                idle_work(op[1], spare[taken[0]])
             elif k == "T":
                 transposes(w[op[1]])
             elif k == "E":

@@ -20,26 +20,25 @@ FLOPS = 2 * TOK * D * 8 * D
 
 RAWB = 10
 GRPB = 5
-WCB = 9
-WARM0 = 6
-WARM1 = 1
+WCB = 7
+WARM0 = 0
+WARM1 = 0
 POOL_OPS = ()
 TAIL = (
-    ("Q", 1), ("D", 2), ("tanh",), ("T", 2), ("sigz",),
-    ("E", 2, "SS"), ("T", 6), ("D", 1), ("E", 6, "SS"), ("blend",),
-    ("Q", 2), ("T", 7), ("Q", 6), ("E", 7, "SS"), ("F", 0),
-    ("T", 3), ("F", 1), ("D", 2), ("st", 0), ("sq", 0),
-    ("F", 2), ("st", 1), ("E", 3, "SS"), ("nm", 0, "SS"), ("sq", 1),
-    ("st", 2), ("T", 5), ("Q", 7), ("Q", 3), ("D", 1),
-    ("sq", 2), ("F", 3), ("nm", 1, "SS"), ("nm", 2, "SS"), ("D", 2),
-    ("st", 3), ("T", 4), ("sq", 3), ("E", 5, "SV"), ("B", 1),
-    ("D", 1), ("B", 0), ("af", 1, "SV"), ("nm", 3, "SV"), ("D", 2),
-    ("rg", 1), ("B", 3), ("af", 0, "SS"), ("E", 4, "VS"), ("B", 2),
-    ("P", 1, 0), ("rg", 0), ("Q", 5), ("P", 0, 0), ("Q", 4),
-    ("af", 2, "SV"), ("oe", 1, 0, "SS"), ("rg", 2), ("af", 3, "VV"), ("rg", 3),
-    ("oe", 0, 0, "SS"), ("P", 0, 1), ("P", 1, 1), ("oe", 0, 1, "SS"), ("oe", 1, 1, "SS"),
-    ("P", 2, 1), ("P", 2, 0), ("oe", 2, 1, "SS"), ("P", 3, 1), ("P", 3, 0),
-    ("oe", 2, 0, "VV"), ("oe", 3, 1, "VS"), ("oe", 3, 0, "SS"),
+    ("T", 2), ("tanh",), ("T", 6), ("Q", 1), ("sigz",),
+    ("blend",), ("T", 7), ("E", 2, "SS"), ("T", 3), ("E", 7, "SS"),
+    ("E", 3, "VS"), ("T", 5), ("F", 0), ("Q", 2), ("st", 0),
+    ("F", 1), ("E", 6, "SS"), ("F", 2), ("sq", 0), ("st", 1),
+    ("st", 2), ("E", 5, "SS"), ("Q", 3), ("sq", 1), ("nm", 0, "SS"),
+    ("sq", 2), ("T", 4), ("nm", 1, "SS"), ("B", 0), ("af", 0, "SS"),
+    ("F", 3), ("nm", 2, "SS"), ("E", 4, "VS"), ("st", 3), ("rg", 0),
+    ("B", 1), ("af", 1, "VV"), ("B", 2), ("P", 0, 0), ("rg", 1),
+    ("P", 1, 0), ("sq", 3), ("af", 2, "SS"), ("nm", 3, "SS"), ("rg", 2),
+    ("Q", 5), ("oe", 0, 0, "SS"), ("oe", 1, 0, "SS"), ("P", 2, 0), ("B", 3),
+    ("Q", 4), ("oe", 2, 0, "SS"), ("Q", 7), ("Q", 6), ("P", 2, 1),
+    ("af", 3, "VV"), ("oe", 2, 1, "SS"), ("P", 1, 1), ("rg", 3), ("oe", 1, 1, "SS"),
+    ("P", 0, 1), ("P", 3, 0), ("oe", 0, 1, "VV"), ("P", 3, 1), ("oe", 3, 0, "SV"),
+    ("oe", 3, 1, "SV"),
 )
 
 
@@ -55,7 +54,7 @@ def tile_instrumentspecificslotmemory_pb_kernel(
         wcp = ctx.enter_context(tc.tile_pool(name="wcp", bufs=WCB))
         work = ctx.enter_context(tc.tile_pool(name="work", bufs=2))
         lnp = ctx.enter_context(tc.tile_pool(name="lnp", bufs=4))
-        outp = ctx.enter_context(tc.tile_pool(name="outp", bufs=6))
+        outp = ctx.enter_context(tc.tile_pool(name="outp", bufs=8))
         psum = ctx.enter_context(tc.psum_pool(name="psum", bufs=1))
 
         spare = [0, 1, 2, 3, 4, 5, 6]
@@ -111,7 +110,7 @@ def tile_instrumentspecificslotmemory_pb_kernel(
         nc.scalar.dma_start(out=braw[24:28, :], in_=g_mem.rearrange("(a w) -> a w", w=256))
         nc.scalar.dma_start(out=braw[28:32, :], in_=b_mem.rearrange("(a w) -> a w", w=256))
         zt = const.tile([P, TOK], BF16, name="zt")
-        nc.vector.memset(zt[:], 1.0)
+        nc.vector.memset(zt[:].bitcast(I32), 0)
         for i in range(RAWB):
             load()
         eps_t = const.tile([P, 1], F32, name="eps_t")
@@ -212,8 +211,8 @@ def tile_instrumentspecificslotmemory_pb_kernel(
 
         tl = {}
 
-        def ew(name):
-            return nc.gpsimd if name in POOL_OPS else nc.vector
+        def ew(j):
+            return nc.gpsimd if j < 7 else nc.vector
 
         def sig_r(j):
             tl[("r", j)] = work.tile([P, TOK], F32, name="r", tag="r")
@@ -240,12 +239,12 @@ def tile_instrumentspecificslotmemory_pb_kernel(
             d = work.tile([P, TOK], F32, name="d", tag="d")
             tl[("d", j)] = d
             m = a_grp[("mo", j // 4)][:].rearrange("p (k t) -> p k t", t=4)[:, :, j % 4]
-            ew("sub").tensor_tensor(out=d[:], in0=m, in1=tl[("n", j)][:], op=ALU.subtract)
+            ew(j).tensor_tensor(out=d[:], in0=m, in1=tl[("n", j)][:], op=ALU.subtract)
 
         def blend_rest(j):
             d = tl[("d", j)]
-            ew("mul").tensor_tensor(out=d[:], in0=d[:], in1=tl[("z", j)][:], op=ALU.mult)
-            ew("add").tensor_tensor(out=hT[:, j, :], in0=d[:], in1=tl[("n", j)][:], op=ALU.add)
+            ew(j).tensor_tensor(out=d[:], in0=d[:], in1=tl[("z", j)][:], op=ALU.mult)
+            ew(j).tensor_tensor(out=hT[:, j, :], in0=d[:], in1=tl[("n", j)][:], op=ALU.add)
 
         hb = {}
         mv = {}
@@ -336,9 +335,9 @@ def tile_instrumentspecificslotmemory_pb_kernel(
                 give(("P", tt, m, h))
                 nc.sync.dma_start(out=outs[m][tt * P : (tt + 1) * P, h * TOK : (h + 1) * TOK], in_=osb[:])
 
-        def idle_work(n, b=6):
+        def idle_work(n):
             for i in range(n):
-                bk = bank("idle", [P, TOK], b)
+                bk = bank("idle", [P, TOK], 6)
                 nc.tensor.matmul(out=bk[:], lhsT=zt[:, 0:P], rhs=zt[:], start=True, stop=True)
 
         idle_work(WARM0)
@@ -373,7 +372,7 @@ def tile_instrumentspecificslotmemory_pb_kernel(
                 blend_sub(j - 1)
                 blend_rest(j - 1)
                 evacuate(c3, 0, "S")
-                evacuate(c3, 1, "S")
+                evacuate(c3, 1, "V")
             sig_r(j)
             if j > 0:
                 quantise(c3)
@@ -408,8 +407,6 @@ def tile_instrumentspecificslotmemory_pb_kernel(
             elif k == "blend":
                 blend_sub(7)
                 blend_rest(7)
-            elif k == "D":
-                idle_work(op[1], spare[taken[0]])
             elif k == "T":
                 transposes(w[op[1]])
             elif k == "E":

@@ -126,8 +126,8 @@ def tile_instrumentspecificslotmemory_pb_kernel(
         w2c = const.tile([P, 2, 2, 2, TOK], U32, name="w2c", align_bytes=64)
         w2s = const.tile([P, 2, 2, 2, TOK], U8, name="w2s", align_bytes=64)
         hT = const.tile([P, 8, TOK], F32, name="hT")
-        m2c = const.tile([P, 2, TOK], U32, name="m2c", align_bytes=64)
-        m2s = const.tile([P, 2, TOK], U8, name="m2s", align_bytes=64)
+        m2c = const.tile([P, 4, 2 * P], U32, name="m2c", align_bytes=64)
+        m2s = const.tile([P, 4, 2 * P], U8, name="m2s", align_bytes=64)
 
         banks = {}
         grp = {}
@@ -268,10 +268,10 @@ def tile_instrumentspecificslotmemory_pb_kernel(
                 nc.vector.bn_stats(out=st[:, half, :], in_=hb[(tt, half)][:])
             mv[tt] = lnp.tile([P, 2], F32, name="mv", tag="mv")
             nc.vector.bn_aggr(out=mv[tt][:], in_=st[:].rearrange("p a b -> p (a b)"))
-            ve[tt] = lnp.tile([P, 1], F32, name="ve", tag="ve")
-            nc.vector.tensor_scalar(out=ve[tt][:], in0=mv[tt][:, 1:2], scalar1=EPS, scalar2=None, op0=ALU.add)
 
         def root(tt):
+            ve[tt] = lnp.tile([P, 1], F32, name="ve", tag="ve")
+            nc.gpsimd.tensor_scalar(out=ve[tt][:], in0=mv[tt][:, 1:2], scalar1=EPS, scalar2=None, op0=ALU.add)
             rstd[tt] = lnp.tile([P, 1], F32, name="rstd", tag="rstd")
             nc.gpsimd.tensor_tensor(out=rstd[tt][:], in0=ve[tt][:], in1=mhalf[:], op=ALU.pow)
             nmr[tt] = lnp.tile([P, 1], F32, name="nmr", tag="nmr")
@@ -305,12 +305,19 @@ def tile_instrumentspecificslotmemory_pb_kernel(
                     nc.vector.tensor_scalar(out=mn[tt][:, j, :], in0=bb[(tt, g)][:, t, :], scalar1=bf[:, 48 + j : 49 + j], scalar2=bf[:, 56 + j : 57 + j], op0=ALU.mult, op1=ALU.add)
             give(("B", tt, g))
 
-        def regroup(tt, g):
-            g2 = lnp.tile([P, 4 * P], BF16, name="g2", tag="g2", align_bytes=64)
-            nc.vector.tensor_copy(out=g2[:].rearrange("p (k t) -> p k t", t=4), in_=mn[tt][:, 4 * g : 4 * g + 4, :].rearrange("p t k -> p k t"))
-            cols = slice(tt * P, (tt + 1) * P)
-            nc.vector.quantize_mx(out=m2c[:, g, cols].bitcast(FP8X4), scales=m2s[:, g, cols], in_=g2[:])
+        def regroup(tt):
+            g2 = lnp.tile([P, 8 * P], BF16, name="g2", tag="g2", align_bytes=64)
+            for g in range(2):
+                nc.vector.tensor_copy(
+                    out=g2[:, g * 512 : (g + 1) * 512].rearrange("p (k t) -> p k t", t=4),
+                    in_=mn[tt][:, 4 * g : 4 * g + 4, :].rearrange("p t k -> p k t"),
+                )
+            gq[tt] = g2
 
+        def quant2(tt):
+            nc.vector.quantize_mx(out=m2c[:, tt, :].bitcast(FP8X4), scales=m2s[:, tt, :], in_=gq[tt][:])
+
+        gq = {}
         pb = {}
 
         def project(tt, m):
@@ -319,8 +326,8 @@ def tile_instrumentspecificslotmemory_pb_kernel(
                 for g in range(2):
                     nc.tensor.matmul_mx(
                         out=bk[:],
-                        lhsT=m2c[:, g, tt * P : (tt + 1) * P].bitcast(FP8X4),
-                        lhsT_scale=m2s[:, g, tt * P : (tt + 1) * P],
+                        lhsT=m2c[:, tt, g * P : (g + 1) * P].bitcast(FP8X4),
+                        lhsT_scale=m2s[:, tt, g * P : (g + 1) * P],
                         rhs=w2c[:, m, g, h, :].bitcast(FP8X4),
                         rhs_scale=w2s[:, m, g, h, :],
                         start=(g == 0),
@@ -405,8 +412,16 @@ def tile_instrumentspecificslotmemory_pb_kernel(
                 sig_z(7)
                 give(("z", 7))
             elif k == "blend":
-                blend_sub(7)
-                blend_rest(7)
+                d = work.tile([P, TOK], F32, name="d", tag="d")
+                m = a_grp[("mo", 1)][:].rearrange("p (k t) -> p k t", t=4)[:, :, 3]
+                n, z = tl[("n", 7)], tl[("z", 7)]
+                halves = (slice(0, 256), slice(256, TOK))
+                for c in halves:
+                    nc.vector.tensor_tensor(out=d[:, c], in0=m[:, c], in1=n[:, c], op=ALU.subtract)
+                for c in halves:
+                    nc.vector.tensor_tensor(out=d[:, c], in0=d[:, c], in1=z[:, c], op=ALU.mult)
+                for c in halves:
+                    nc.vector.tensor_tensor(out=hT[:, 7, c], in0=d[:, c], in1=n[:, c], op=ALU.add)
             elif k == "T":
                 transposes(w[op[1]])
             elif k == "E":
@@ -428,8 +443,8 @@ def tile_instrumentspecificslotmemory_pb_kernel(
                 affine(op[1], 0, op[2][0] * 4)
                 affine(op[1], 1, op[2][1] * 4)
             elif k == "rg":
-                regroup(op[1], 0)
-                regroup(op[1], 1)
+                regroup(op[1])
+                quant2(op[1])
             elif k == "P":
                 project(op[1], op[2])
             else:

@@ -21,8 +21,8 @@ FLOPS = 2 * TOK * D * 8 * D
 RAWB = 10
 GRPB = 5
 WCB = 7
-WARM0 = 0
-WARM1 = 0
+WARM0 = 6
+WARM1 = 1
 POOL_OPS = ()
 TAIL = (
     ("T", 2), ("tanh",), ("T", 6), ("Q", 1), ("sigz",),

@@ -21,8 +21,11 @@ FLOPS = 2 * TOK * D * 8 * D
 RAWB = 10
 GRPB = 5
 WCB = 7
+BI = 5
 WARM0 = 6
-WARM1 = 1
+HEAD = (("agg", 0), ("agg", 1), ("mo", 0), ("mo", 1), (0, 0), (2, 0), (1, 0))
+HE = ("SV", "SV", "SV", "SV", "SV", "SS", "SV")
+WH = (1, 1, 1, 1, 1, 1, 0)
 POOL_OPS = ()
 TAIL = (
     ("T", 2), ("tanh",), ("T", 6), ("Q", 1), ("sigz",),
@@ -83,7 +86,7 @@ def tile_instrumentspecificslotmemory_pb_kernel(
         outs = [out_0.flatten_outer_dims(), out_1.flatten_outer_dims()]
 
         stream = [(q, j) for j in range(8) for q in (0, 2, 1)] + [("w2", m, ci) for m in range(2) for ci in range(4)]
-        names = [("agg", 0), ("agg", 1), ("mo", 0), ("mo", 1)] + stream
+        names = list(HEAD) + stream[3:]
 
         raw = {}
 
@@ -347,28 +350,25 @@ def tile_instrumentspecificslotmemory_pb_kernel(
                 bk = bank("idle", [P, TOK], 6)
                 nc.tensor.matmul(out=bk[:], lhsT=zt[:, 0:P], rhs=zt[:], start=True, stop=True)
 
-        idle_work(WARM0)
-        for i, (x, th) in enumerate((("agg", 0), ("agg", 1), ("mo", 0), ("mo", 1))):
-            transposes((x, th), (2 * i) % 6)
-            idle_work(WARM1)
-            evacuate((x, th), 0, "S")
-            evacuate((x, th), 1, "V")
-            quantise_act(x, 0, th)
-            quantise_act(x, 1, th)
-        tb = [1]
+        tb = [0]
 
         def tr(nm):
             transposes(nm, 2 * (tb[0] % 2))
             tb[0] += 1
 
-        for nm in stream[:3]:
+        idle_work(WARM0)
+        for i, nm in enumerate(HEAD):
             tr(nm)
-            idle_work(WARM1)
-            if nm == stream[0]:
+            idle_work(WH[i])
+            evacuate(nm, 0, HE[i][0])
+            evacuate(nm, 1, HE[i][1])
+            if nm[0] in ("agg", "mo"):
+                quantise_act(nm[0], 0, nm[1])
+                quantise_act(nm[0], 1, nm[1])
+            else:
+                quantise(nm)
+            if i == BI:
                 biases(7)
-            evacuate(nm, 0, "S")
-            evacuate(nm, 1, "V")
-            quantise(nm)
 
         c3 = None
         for j in range(8):

@@ -28,20 +28,97 @@ HE = ("SV", "SV", "SV", "SV", "SV", "SS", "SV")
 WH = (1, 1, 1, 1, 1, 1, 0)
 POOL_OPS = ()
 TAIL = (
-    ("T", 2), ("tanh",), ("T", 6), ("Q", 1), ("sigz",),
-    ("blend",), ("T", 7), ("E", 2, "SS"), ("T", 3), ("E", 7, "SS"),
-    ("E", 3, "VS"), ("T", 5), ("F", 0), ("Q", 2), ("st", 0),
-    ("F", 1), ("E", 6, "SS"), ("F", 2), ("sq", 0), ("st", 1),
-    ("st", 2), ("E", 5, "SS"), ("Q", 3), ("sq", 1), ("nm", 0, "SS"),
-    ("sq", 2), ("T", 4), ("nm", 1, "SS"), ("B", 0), ("af", 0, "SS"),
-    ("F", 3), ("nm", 2, "SS"), ("E", 4, "VS"), ("st", 3), ("rg", 0),
-    ("B", 1), ("af", 1, "VV"), ("B", 2), ("P", 0, 0), ("rg", 1),
-    ("P", 1, 0), ("sq", 3), ("af", 2, "SS"), ("nm", 3, "SS"), ("rg", 2),
-    ("Q", 5), ("oe", 0, 0, "SS"), ("oe", 1, 0, "SS"), ("P", 2, 0), ("B", 3),
-    ("Q", 4), ("oe", 2, 0, "SS"), ("Q", 7), ("Q", 6), ("P", 2, 1),
-    ("af", 3, "VV"), ("oe", 2, 1, "SS"), ("P", 1, 1), ("rg", 3), ("oe", 1, 1, "SS"),
-    ("P", 0, 1), ("P", 3, 0), ("oe", 0, 1, "VV"), ("P", 3, 1), ("oe", 3, 0, "SV"),
-    ("oe", 3, 1, "SV"),
+    ("T", 2),
+    ("T", 6),
+    ("tanh",),
+    ("sigz",),
+    ("T", 7),
+    ("Q", 1),
+    ("blend",),
+    ("E", 2, "SS"),
+    ("F", 0),
+    ("F", 1),
+    ("E", 6, "SS"),
+    ("T", 3),
+    ("E", 7, "SS"),
+    ("F", 2),
+    ("E", 3, "SS"),
+    ("F", 3),
+    ("st", 0),
+    ("Q", 2, 0),
+    ("ag", 0),
+    ("Q", 2, 1),
+    ("ve", 0),
+    ("sq", 0),
+    ("st", 1),
+    ("Q", 6, 0),
+    ("ag", 1),
+    ("Q", 6, 1),
+    ("ve", 1),
+    ("sq", 1),
+    ("st", 2),
+    ("s", 3),
+    ("ag", 2),
+    ("st", 3),
+    ("ve", 2),
+    ("sq", 2),
+    ("Q", 3, 0),
+    ("ag", 3),
+    ("Q", 3, 1),
+    ("ve", 3),
+    ("sq", 3),
+    ("nm", 0, "SS"),
+    ("B", 0),
+    ("nm", 1, "SS"),
+    ("B", 1),
+    ("af", 0, "SV"),
+    ("T", 5),
+    ("nm", 2, "SS"),
+    ("Q", 7, 0),
+    ("rg", 0),
+    ("Q", 7, 1),
+    ("af", 1, "SV"),
+    ("B", 2),
+    ("E", 5, "SS"),
+    ("q2", 0),
+    ("P", 0, 0),
+    ("rg", 1),
+    ("nm", 3, "VV"),
+    ("q2", 1),
+    ("af", 2, "SV"),
+    ("B", 3),
+    ("P", 0, 1, 1),
+    ("oe", 0, 0, "SS"),
+    ("P", 1, 0),
+    ("rg", 2),
+    ("af", 3, "SV"),
+    ("q2", 2),
+    ("T", 4),
+    ("oe", 0, 1, 1, "S"),
+    ("P", 1, 1, 1),
+    ("rg", 3),
+    ("Q", 5),
+    ("q2", 3),
+    ("P", 2, 0),
+    ("oe", 1, 0, "SV"),
+    ("E", 4, "SS"),
+    ("P", 2, 1, 1),
+    ("oe", 1, 1, 1, "S"),
+    ("P", 3, 0),
+    ("Q", 4),
+    ("oe", 2, 0, "SV"),
+    ("P", 3, 1, 1),
+    ("P", 0, 1, 0),
+    ("oe", 2, 1, 1, "S"),
+    ("P", 1, 1, 0),
+    ("oe", 3, 0, "VS"),
+    ("P", 2, 1, 0),
+    ("oe", 3, 1, 1, "V"),
+    ("P", 3, 1, 0),
+    ("oe", 0, 1, 0, "S"),
+    ("oe", 1, 1, 0, "V"),
+    ("oe", 2, 1, 0, "S"),
+    ("oe", 3, 1, 0, "V"),
 )
 
 
@@ -164,11 +241,11 @@ def tile_instrumentspecificslotmemory_pb_kernel(
             cols = slice(th * 256, (th + 1) * 256)
             nc.vector.quantize_mx(out=a_c[x][:, g, cols].bitcast(FP8X4), scales=a_s[x][:, g, cols], in_=a_grp[(x, g)][:, th * 1024 : (th + 1) * 1024])
 
-        def quantise(nm):
+        def quantise(nm, gs=(0, 1)):
             if nm[0] == "w2":
                 m, ci = nm[1], nm[2]
                 h, cp = ci // 2, ci % 2
-                for g in range(2):
+                for g in gs:
                     nc.vector.quantize_mx(
                         out=w2c[:, m, g, h, cp * 256 : (cp + 1) * 256].bitcast(FP8X4),
                         scales=w2s[:, m, g, h, cp * 256 : (cp + 1) * 256],
@@ -258,23 +335,28 @@ def tile_instrumentspecificslotmemory_pb_kernel(
         bb = {}
         mn = {}
 
-        def fwd(tt):
-            for half in range(2):
-                bk = bank(("F", tt, half), [P, TOK])
-                for jj in range(4):
-                    nc.tensor.transpose(bk[:, jj * P : (jj + 1) * P], hT[:, 4 * half + jj, tt * P : (tt + 1) * P], ident[:])
-                hb[(tt, half)] = bk
+        def fwd(tt, half):
+            bk = bank(("F", tt, half), [P, TOK])
+            for jj in range(4):
+                nc.tensor.transpose(bk[:, jj * P : (jj + 1) * P], hT[:, 4 * half + jj, tt * P : (tt + 1) * P], ident[:])
+            hb[(tt, half)] = bk
 
-        def stats(tt):
-            st = lnp.tile([P, 2, 6], F32, name="st", tag="st")
-            for half in range(2):
-                nc.vector.bn_stats(out=st[:, half, :], in_=hb[(tt, half)][:])
+        def stats(tt, half):
+            if tt not in sts:
+                sts[tt] = lnp.tile([P, 2, 6], F32, name="st", tag="st")
+            nc.vector.bn_stats(out=sts[tt][:, half, :], in_=hb[(tt, half)][:])
+
+        sts = {}
+
+        def aggr(tt):
             mv[tt] = lnp.tile([P, 2], F32, name="mv", tag="mv")
-            nc.vector.bn_aggr(out=mv[tt][:], in_=st[:].rearrange("p a b -> p (a b)"))
+            nc.vector.bn_aggr(out=mv[tt][:], in_=sts[tt][:].rearrange("p a b -> p (a b)"))
+
+        def eps(tt):
+            ve[tt] = lnp.tile([P, 1], F32, name="ve", tag="ve")
+            nc.vector.tensor_scalar(out=ve[tt][:], in0=mv[tt][:, 1:2], scalar1=EPS, scalar2=None, op0=ALU.add)
 
         def root(tt):
-            ve[tt] = lnp.tile([P, 1], F32, name="ve", tag="ve")
-            nc.gpsimd.tensor_scalar(out=ve[tt][:], in0=mv[tt][:, 1:2], scalar1=EPS, scalar2=None, op0=ALU.add)
             rstd[tt] = lnp.tile([P, 1], F32, name="rstd", tag="rstd")
             nc.gpsimd.tensor_tensor(out=rstd[tt][:], in0=ve[tt][:], in1=mhalf[:], op=ALU.pow)
             nmr[tt] = lnp.tile([P, 1], F32, name="nmr", tag="nmr")
@@ -323,8 +405,8 @@ def tile_instrumentspecificslotmemory_pb_kernel(
         gq = {}
         pb = {}
 
-        def project(tt, m):
-            for h in range(2):
+        def project(tt, m, hs=(0, 1)):
+            for h in hs:
                 bk = bank(("P", tt, m, h), [P, TOK])
                 for g in range(2):
                     nc.tensor.matmul_mx(
@@ -338,8 +420,8 @@ def tile_instrumentspecificslotmemory_pb_kernel(
                     )
                 pb[(tt, m, h)] = bk
 
-        def results(tt, m, engs):
-            for h in range(2):
+        def results(tt, m, engs, hs=(0, 1)):
+            for h in hs:
                 osb = outp.tile([P, TOK], F32, name="osb", tag="osb")
                 copy_on(engs[h])(out=osb[:], in_=pb[(tt, m, h)][:])
                 give(("P", tt, m, h))
@@ -404,35 +486,56 @@ def tile_instrumentspecificslotmemory_pb_kernel(
         w = stream[24:]
         taken[0] = len(spare)
         spare.extend([0, 1, 2, 3, 4, 5, 6])
+        halves = (slice(0, 256), slice(256, TOK))
         for op in TAIL:
             k = op[0]
             if k == "tanh":
-                tanh_n(7)
+                n = tl[("n", 7)] = work.tile([P, TOK], F32, name="n", tag="n")
+                for c in halves:
+                    nc.scalar.activation(out=n[:, c], in_=tl[("t", 7)][:, c], func=ACT.Tanh, bias=bf[:, 23:24], scale=1.0)
             elif k == "sigz":
-                sig_z(7)
+                z = tl[("z", 7)] = work.tile([P, TOK], F32, name="g1", tag="g1")
+                for c in halves:
+                    nc.scalar.activation(out=z[:, c], in_=acc[("z", 7)][:, c], func=ACT.Sigmoid, bias=brz[:, 15:16], scale=1.0)
                 give(("z", 7))
             elif k == "blend":
                 d = work.tile([P, TOK], F32, name="d", tag="d")
                 m = a_grp[("mo", 1)][:].rearrange("p (k t) -> p k t", t=4)[:, :, 3]
                 n, z = tl[("n", 7)], tl[("z", 7)]
-                halves = (slice(0, 256), slice(256, TOK))
                 for c in halves:
                     nc.vector.tensor_tensor(out=d[:, c], in0=m[:, c], in1=n[:, c], op=ALU.subtract)
                 for c in halves:
                     nc.vector.tensor_tensor(out=d[:, c], in0=d[:, c], in1=z[:, c], op=ALU.mult)
                 for c in halves:
                     nc.vector.tensor_tensor(out=hT[:, 7, c], in0=d[:, c], in1=n[:, c], op=ALU.add)
+            elif k == "D":
+                bk = bank(("D", op[2]), [P, TOK])
+                for i in range(op[1]):
+                    nc.tensor.matmul(out=bk[:], lhsT=zt[:, 0:P], rhs=zt[:], start=True, stop=True)
+                give(("D", op[2]))
             elif k == "T":
                 transposes(w[op[1]])
             elif k == "E":
                 evacuate(w[op[1]], 0, op[2][0])
                 evacuate(w[op[1]], 1, op[2][1])
             elif k == "Q":
-                quantise(w[op[1]])
+                quantise(w[op[1]], op[2:] or (0, 1))
             elif k == "F":
-                fwd(op[1])
+                for half in range(2):
+                    if (op[1], half) not in hb:
+                        fwd(op[1], half)
+            elif k == "f":
+                fwd(op[1], 0)
+            elif k == "s":
+                stats(op[1], 0)
             elif k == "st":
-                stats(op[1])
+                if op[1] not in sts:
+                    stats(op[1], 0)
+                stats(op[1], 1)
+            elif k == "ag":
+                aggr(op[1])
+            elif k == "ve":
+                eps(op[1])
             elif k == "sq":
                 root(op[1])
             elif k == "nm":
@@ -444,8 +547,11 @@ def tile_instrumentspecificslotmemory_pb_kernel(
                 affine(op[1], 1, op[2][1] * 4)
             elif k == "rg":
                 regroup(op[1])
+            elif k == "q2":
                 quant2(op[1])
             elif k == "P":
-                project(op[1], op[2])
-            else:
+                project(op[1], op[2], op[3:] or (0, 1))
+            elif len(op) == 4:
                 results(op[1], op[2], op[3])
+            else:
+                results(op[1], op[2], op[4] * 2, (op[3],))

@@ -22,7 +22,7 @@ RAWB = 10
 GRPB = 5
 WCB = 7
 BI = 5
-WARM0 = 6
+WARM0 = 4
 HEAD = (("agg", 0), ("agg", 1), ("mo", 0), ("mo", 1), (0, 0), (2, 0), (1, 0))
 HE = ("SV", "SV", "SV", "SV", "SV", "SS", "SV")
 WH = (1, 1, 1, 1, 1, 1, 0)
@@ -90,13 +90,13 @@ TAIL = (
     ("P", 0, 1, 1),
     ("oe", 0, 0, "SS"),
     ("P", 1, 0),
-    ("rg", 2),
+    ("rg", 2, "G"),
     ("af", 3, "SV"),
+    ("rg", 3),
     ("q2", 2),
     ("T", 4),
     ("oe", 0, 1, 1, "S"),
     ("P", 1, 1, 1),
-    ("rg", 3),
     ("Q", 5),
     ("q2", 3),
     ("P", 2, 0),
@@ -390,13 +390,15 @@ def tile_instrumentspecificslotmemory_pb_kernel(
                     nc.vector.tensor_scalar(out=mn[tt][:, j, :], in0=bb[(tt, g)][:, t, :], scalar1=bf[:, 48 + j : 49 + j], scalar2=bf[:, 56 + j : 57 + j], op0=ALU.mult, op1=ALU.add)
             give(("B", tt, g))
 
-        def regroup(tt):
+        def regroup(tt, eng):
             g2 = lnp.tile([P, 8 * P], BF16, name="g2", tag="g2", align_bytes=64)
             for g in range(2):
-                nc.vector.tensor_copy(
-                    out=g2[:, g * 512 : (g + 1) * 512].rearrange("p (k t) -> p k t", t=4),
-                    in_=mn[tt][:, 4 * g : 4 * g + 4, :].rearrange("p t k -> p k t"),
-                )
+                dst = g2[:, g * 512 : (g + 1) * 512].rearrange("p (k t) -> p k t", t=4)
+                src = mn[tt][:, 4 * g : 4 * g + 4, :].rearrange("p t k -> p k t")
+                if eng == "V":
+                    nc.vector.tensor_copy(out=dst, in_=src)
+                else:
+                    nc.gpsimd.tensor_scalar(out=dst, in0=src, scalar1=1.0, scalar2=0.0, op0=ALU.mult, op1=ALU.add)
             gq[tt] = g2
 
         def quant2(tt):
@@ -546,7 +548,7 @@ def tile_instrumentspecificslotmemory_pb_kernel(
                 affine(op[1], 0, op[2][0] * 4)
                 affine(op[1], 1, op[2][1] * 4)
             elif k == "rg":
-                regroup(op[1])
+                regroup(op[1], op[2] if len(op) == 3 else "V")
             elif k == "q2":
                 quant2(op[1])
             elif k == "P":

@@ -14,112 +14,32 @@ ALU = mybir.AluOpType
 
 P = 128
 D = 1024
-TOK = 512
+SLOTS = 512
+TILES = SLOTS // P
+HALF = SLOTS // 2
+FT = D // P
+LAST = FT - 1
+K4 = 4
+PASSES = D // (K4 * P)
+PAIR = 2 * P
+WORDS = 2 * PAIR
 EPS = 1e-5
-FLOPS = 2 * TOK * D * 8 * D
 
-RAWB = 10
-GRPB = 5
-WCB = 7
-BI = 5
-WARM0 = 4
-HEAD = (("agg", 0), ("agg", 1), ("mo", 0), ("mo", 1), (0, 0), (2, 0), (1, 0))
-HE = ("SV", "SV", "SV", "SV", "SV", "SS", "SV")
-WH = (1, 1, 1, 1, 1, 1, 0)
-POOL_OPS = ()
-TAIL = (
-    ("T", 2),
-    ("T", 6),
-    ("tanh",),
-    ("sigz",),
-    ("T", 7),
-    ("Q", 1),
-    ("blend",),
-    ("E", 2, "SS"),
-    ("F", 0),
-    ("F", 1),
-    ("E", 6, "SS"),
-    ("T", 3),
-    ("E", 7, "SS"),
-    ("F", 2),
-    ("E", 3, "SS"),
-    ("F", 3),
-    ("st", 0),
-    ("Q", 2, 0),
-    ("ag", 0),
-    ("Q", 2, 1),
-    ("ve", 0),
-    ("sq", 0),
-    ("st", 1),
-    ("Q", 6, 0),
-    ("ag", 1),
-    ("Q", 6, 1),
-    ("ve", 1),
-    ("sq", 1),
-    ("st", 2),
-    ("s", 3),
-    ("ag", 2),
-    ("st", 3),
-    ("ve", 2),
-    ("sq", 2),
-    ("Q", 3, 0),
-    ("ag", 3),
-    ("Q", 3, 1),
-    ("ve", 3),
-    ("sq", 3),
-    ("nm", 0, "SS"),
-    ("B", 0),
-    ("nm", 1, "SS"),
-    ("B", 1),
-    ("af", 0, "SV"),
-    ("T", 5),
-    ("nm", 2, "SS"),
-    ("Q", 7, 0),
-    ("rg", 0),
-    ("Q", 7, 1),
-    ("af", 1, "SV"),
-    ("B", 2),
-    ("E", 5, "SS"),
-    ("q2", 0),
-    ("P", 0, 0),
-    ("rg", 1),
-    ("nm", 3, "VV"),
-    ("q2", 1),
-    ("af", 2, "SV"),
-    ("B", 3),
-    ("P", 0, 1, 1),
-    ("oe", 0, 0, "SS"),
-    ("P", 1, 0),
-    ("rg", 2, "G"),
-    ("af", 3, "SV"),
-    ("rg", 3),
-    ("q2", 2),
-    ("T", 4),
-    ("oe", 0, 1, 1, "S"),
-    ("P", 1, 1, 1),
-    ("Q", 5),
-    ("q2", 3),
-    ("P", 2, 0),
-    ("oe", 1, 0, "SV"),
-    ("E", 4, "SS"),
-    ("P", 2, 1, 1),
-    ("oe", 1, 1, 1, "S"),
-    ("P", 3, 0),
-    ("Q", 4),
-    ("oe", 2, 0, "SV"),
-    ("P", 3, 1, 1),
-    ("P", 0, 1, 0),
-    ("oe", 2, 1, 1, "S"),
-    ("P", 1, 1, 0),
-    ("oe", 3, 0, "VS"),
-    ("P", 2, 1, 0),
-    ("oe", 3, 1, 1, "V"),
-    ("P", 3, 1, 0),
-    ("oe", 0, 1, 0, "S"),
-    ("oe", 1, 1, 0, "V"),
-    ("oe", 2, 1, 0, "S"),
-    ("oe", 3, 1, 0, "V"),
-)
+IH_R, IH_N = 0, 2 * FT
+HH_R, HH_N = 3 * FT, 5 * FT
+GAIN, SHIFT = 6 * FT, 7 * FT
+VECTOR_COLUMNS = 8 * FT
+
+R, Z, N = 0, 1, 2
+AGG, MEM = "agg", "mem"
+WP = "wp"
+
+RAW_BUFS = 10
+PAIRED_BUFS = 5
+CODE_BUFS = 7
+GATE_BUFS = 2
+OUT_BUFS = 8
+IDLE_FIRST = 4
 
 
 def tile_instrumentspecificslotmemory_pb_kernel(
@@ -129,431 +49,485 @@ def tile_instrumentspecificslotmemory_pb_kernel(
     with ExitStack() as ctx:
         ctx.enter_context(tc.manual_schedule())
         const = ctx.enter_context(tc.tile_pool(name="const", bufs=1))
-        rawp = ctx.enter_context(tc.tile_pool(name="rawp", bufs=RAWB))
-        grpp = ctx.enter_context(tc.tile_pool(name="grpp", bufs=GRPB))
-        wcp = ctx.enter_context(tc.tile_pool(name="wcp", bufs=WCB))
-        work = ctx.enter_context(tc.tile_pool(name="work", bufs=2))
-        lnp = ctx.enter_context(tc.tile_pool(name="lnp", bufs=4))
-        outp = ctx.enter_context(tc.tile_pool(name="outp", bufs=8))
+        raw_pool = ctx.enter_context(tc.tile_pool(name="raw", bufs=RAW_BUFS))
+        paired_pool = ctx.enter_context(tc.tile_pool(name="paired", bufs=PAIRED_BUFS))
+        code_pool = ctx.enter_context(tc.tile_pool(name="codes", bufs=CODE_BUFS))
+        gate_pool = ctx.enter_context(tc.tile_pool(name="gates", bufs=GATE_BUFS))
+        ln_pool = ctx.enter_context(tc.tile_pool(name="ln", bufs=TILES))
+        out_pool = ctx.enter_context(tc.tile_pool(name="out", bufs=OUT_BUFS))
         psum = ctx.enter_context(tc.psum_pool(name="psum", bufs=1))
 
-        spare = [0, 1, 2, 3, 4, 5, 6]
-        taken = [0]
-        held = {}
+        BIAS_BANK, IDLE_BANK = 7, 6
+        R_BANK, GH_BANK, GI_BANK, Z_BANK = 4, 5, 6, 7
+        free_banks = []
+        next_free = [0]
+        owner = {}
 
-        def bank(key, shape, i=None):
-            if i is None:
-                i = spare[taken[0]]
-                taken[0] += 1
-            held[key] = i
-            return psum.tile(shape, F32, name="b%d" % i, tag="b%d" % i)
+        def bank(key, shape, number=None):
+            if number is None:
+                number = free_banks[next_free[0]]
+                next_free[0] += 1
+            owner[key] = number
+            return psum.tile(shape, F32, name="b%d" % number, tag="b%d" % number)
 
-        def give(key):
-            spare.extend([held[key]])
+        def release(key):
+            free_banks.extend([owner[key]])
 
-        act_v = {
-            "agg": agg.flatten_outer_dims().rearrange("(t p) k -> p t k", p=P),
-            "mo": M_old.flatten_outer_dims().rearrange("(t p) k -> p t k", p=P),
+        act_rows = {
+            AGG: agg.flatten_outer_dims().rearrange("(t p) k -> p t k", p=P),
+            MEM: M_old.flatten_outer_dims().rearrange("(t p) k -> p t k", p=P),
         }
-        w1_v = {
-            "ih": W_ih.rearrange("(a p e) k -> p a e k", p=P, e=2),
-            "hh": W_hh.rearrange("(a p e) k -> p a e k", p=P, e=2),
-        }
-        w2_v = [Wk.rearrange("(j p) k -> p j k", p=P), Wv.rearrange("(j p) k -> p j k", p=P)]
+        gate_rows = [x.rearrange("(a p e) k -> p a e k", p=P, e=2) for x in (W_ih, W_hh)]
+        proj_rows = [x.rearrange("(j p) k -> p j k", p=P) for x in (Wk, Wv)]
         outs = [out_0.flatten_outer_dims(), out_1.flatten_outer_dims()]
 
-        stream = [(q, j) for j in range(8) for q in (0, 2, 1)] + [("w2", m, ci) for m in range(2) for ci in range(4)]
-        names = list(HEAD) + stream[3:]
-
+        activations = [(x, half) for x in (AGG, MEM) for half in range(2)]
+        gate_chunks = [(q, j) for j in range(FT) for q in (R, N, Z)]
+        proj_chunks = [(WP, m, c) for m in range(2) for c in range(D // PAIR)]
+        chunks = gate_chunks + proj_chunks
+        loads = activations + chunks
         raw = {}
 
         def load():
-            if len(raw) < len(names):
-                nm = names[len(raw)]
-                t = rawp.tile([P, 2, D], BF16, name="raw", tag="raw")
-                if nm[0] == "w2":
-                    nc.sync.dma_start(out=t[:], in_=w2_v[nm[1]][:, 2 * nm[2] : 2 * nm[2] + 2, :])
-                elif nm[0] in ("agg", "mo"):
-                    nc.sync.dma_start(out=t[:], in_=act_v[nm[0]][:, 2 * nm[1] : 2 * nm[1] + 2, :])
+            if len(raw) < len(loads):
+                name = loads[len(raw)]
+                tile = raw_pool.tile([P, 2, D], BF16, name="raw", tag="raw")
+                if name[0] == WP:
+                    nc.sync.dma_start(out=tile[:], in_=proj_rows[name[1]][:, 2 * name[2] : 2 * name[2] + 2, :])
+                elif name[0] in act_rows:
+                    nc.sync.dma_start(out=tile[:], in_=act_rows[name[0]][:, 2 * name[1] : 2 * name[1] + 2, :])
                 else:
-                    q, j = nm
-                    for i, x in enumerate(("ih", "hh")):
-                        nc.sync.dma_start(out=t[:, i, :], in_=w1_v[x][:, 4 * q + j // 2, j % 2, :])
-                raw[nm] = t
+                    q, j = name
+                    for x in range(2):
+                        nc.sync.dma_start(out=tile[:, x, :], in_=gate_rows[x][:, q * FT // 2 + j // 2, j % 2, :])
+                raw[name] = tile
 
         ident = const.tile([P, P], F32, name="ident")
         masks.make_identity(nc, ident[:])
-        braw = const.tile([P, 256], BF16, name="braw")
-        nc.vector.memset(braw[:].bitcast(I32), 0)
-        nc.scalar.dma_start(out=braw[0:12, :], in_=b_ih.rearrange("(a w) -> a w", w=256))
-        nc.scalar.dma_start(out=braw[12:24, :], in_=b_hh.rearrange("(a w) -> a w", w=256))
-        nc.scalar.dma_start(out=braw[24:28, :], in_=g_mem.rearrange("(a w) -> a w", w=256))
-        nc.scalar.dma_start(out=braw[28:32, :], in_=b_mem.rearrange("(a w) -> a w", w=256))
-        zt = const.tile([P, TOK], BF16, name="zt")
-        nc.vector.memset(zt[:].bitcast(I32), 0)
-        for i in range(RAWB):
+        vectors = const.tile([P, PAIR], BF16, name="vectors")
+        nc.vector.memset(vectors[:].bitcast(I32), 0)
+        row = 0
+        for vector, length in ((b_ih, 3 * D), (b_hh, 3 * D), (g_mem, D), (b_mem, D)):
+            rows = length // PAIR
+            nc.scalar.dma_start(out=vectors[row : row + rows, :], in_=vector.rearrange("(a w) -> a w", w=PAIR))
+            row += rows
+        zeros = const.tile([P, SLOTS], BF16, name="zeros")
+        nc.vector.memset(zeros[:].bitcast(I32), 0)
+        for i in range(RAW_BUFS):
             load()
-        eps_t = const.tile([P, 1], F32, name="eps_t")
-        nc.vector.memset(eps_t[:], EPS)
-        mhalf = const.tile([P, 1], F32, name="mhalf")
-        nc.vector.memset(mhalf[:], -0.5)
-        warm = const.tile([P, 1], F32, name="warm")
-        nc.scalar.activation(out=warm[:], in_=eps_t[:], func=ACT.Sigmoid)
+        minus_half = const.tile([P, 1], F32, name="minus_half")
+        nc.vector.memset(minus_half[:], -0.5)
+        table = const.tile([P, 1], F32, name="table")
+        nc.scalar.activation(out=table[:], in_=minus_half[:], func=ACT.Sigmoid)
 
-        a_grp = {(x, g): const.tile([P, 4 * TOK], BF16, name="agrp_%s%d" % (x, g), align_bytes=64) for x in ("agg", "mo") for g in range(2)}
-        a_c = {x: const.tile([P, 2, TOK], U32, name="ac_" + x, align_bytes=64) for x in ("agg", "mo")}
-        a_s = {x: const.tile([P, 2, TOK], U8, name="as_" + x, align_bytes=64) for x in ("agg", "mo")}
-        w2c = const.tile([P, 2, 2, 2, TOK], U32, name="w2c", align_bytes=64)
-        w2s = const.tile([P, 2, 2, 2, TOK], U8, name="w2s", align_bytes=64)
-        hT = const.tile([P, 8, TOK], F32, name="hT")
-        m2c = const.tile([P, 4, 2 * P], U32, name="m2c", align_bytes=64)
-        m2s = const.tile([P, 4, 2 * P], U8, name="m2s", align_bytes=64)
+        act_paired = {
+            (x, g): const.tile([P, K4 * SLOTS], BF16, name="paired_%s%d" % (x, g), align_bytes=64)
+            for x in act_rows
+            for g in range(PASSES)
+        }
+        act_codes = {x: const.tile([P, PASSES, SLOTS], U32, name="codes_" + x, align_bytes=64) for x in act_rows}
+        act_scales = {x: const.tile([P, PASSES, SLOTS], U8, name="scales_" + x, align_bytes=64) for x in act_rows}
+        proj_codes = const.tile([P, 2, PASSES, 2, D // 2], U32, name="proj_codes", align_bytes=64)
+        proj_scales = const.tile([P, 2, PASSES, 2, D // 2], U8, name="proj_scales", align_bytes=64)
+        hidden = const.tile([P, FT, SLOTS], F32, name="hidden")
+        memory_codes = const.tile([P, TILES, PASSES * P], U32, name="memory_codes", align_bytes=64)
+        memory_scales = const.tile([P, TILES, PASSES * P], U8, name="memory_scales", align_bytes=64)
 
-        banks = {}
-        grp = {}
-        wc = {}
-        ws = {}
+        def copy_on(engine):
+            return nc.scalar.copy if engine == "S" else nc.vector.tensor_copy
 
-        def copy_on(eng):
-            return nc.scalar.copy if eng == "S" else nc.vector.tensor_copy
+        turned = {}
+        paired = {}
+        codes = {}
+        scales = {}
 
-        def transposes(nm, b=None):
-            words = raw[nm][:].bitcast(F32)
-            for g in range(2):
-                bk = bank((nm, g), [P, 2, 256], None if b is None else b + g)
+        def transpose_load(name, first_bank=None):
+            words = raw[name][:].bitcast(F32)
+            for g in range(PASSES):
+                out = bank((name, g), [P, 2, PAIR], None if first_bank is None else first_bank + g)
                 for u in range(2):
                     for s in range(2):
-                        nc.tensor.transpose(bk[:, u, s * P : (s + 1) * P], words[:, s, (2 * g + u) * P : (2 * g + u + 1) * P], ident[:])
-                banks[(nm, g)] = bk
+                        block = words[:, s, (2 * g + u) * P : (2 * g + u + 1) * P]
+                        nc.tensor.transpose(out[:, u, s * P : (s + 1) * P], block, ident[:])
+                turned[(name, g)] = out
             load()
 
-        def evacuate(nm, g, eng):
-            if nm[0] in ("agg", "mo"):
-                dest = a_grp[(nm[0], g)][:].bitcast(F32)[:, nm[1] * 512 : (nm[1] + 1) * 512]
+        def copy_pass(name, g, engine):
+            if name[0] in act_rows:
+                dest = act_paired[(name[0], g)][:].bitcast(F32)[:, name[1] * WORDS : (name[1] + 1) * WORDS]
             else:
-                if nm not in grp:
-                    grp[nm] = grpp.tile([P, 2048], BF16, name="grp", tag="grp", align_bytes=64)
-                dest = grp[nm][:].bitcast(F32)[:, g * 512 : (g + 1) * 512]
-            copy_on(eng)(out=dest.rearrange("p (o u) -> p o u", u=2), in_=banks[(nm, g)][:].rearrange("p u o -> p o u"))
-            give((nm, g))
+                if name not in paired:
+                    paired[name] = paired_pool.tile([P, PASSES * K4 * PAIR], BF16, name="paired", tag="paired", align_bytes=64)
+                dest = paired[name][:].bitcast(F32)[:, g * WORDS : (g + 1) * WORDS]
+            source = turned[(name, g)][:].rearrange("p u o -> p o u")
+            copy_on(engine)(out=dest.rearrange("p (o u) -> p o u", u=2), in_=source)
+            release((name, g))
 
-        def quantise_act(x, g, th):
-            cols = slice(th * 256, (th + 1) * 256)
-            nc.vector.quantize_mx(out=a_c[x][:, g, cols].bitcast(FP8X4), scales=a_s[x][:, g, cols], in_=a_grp[(x, g)][:, th * 1024 : (th + 1) * 1024])
+        def copy_load(name, engines):
+            for g in range(PASSES):
+                copy_pass(name, g, engines[g])
 
-        def quantise(nm, gs=(0, 1)):
-            if nm[0] == "w2":
-                m, ci = nm[1], nm[2]
-                h, cp = ci // 2, ci % 2
-                for g in gs:
-                    nc.vector.quantize_mx(
-                        out=w2c[:, m, g, h, cp * 256 : (cp + 1) * 256].bitcast(FP8X4),
-                        scales=w2s[:, m, g, h, cp * 256 : (cp + 1) * 256],
-                        in_=grp[nm][:, g * 1024 : (g + 1) * 1024],
-                    )
+        def quantise_activation(name):
+            x, half = name
+            cols = slice(half * HALF, (half + 1) * HALF)
+            for g in range(PASSES):
+                nc.vector.quantize_mx(
+                    out=act_codes[x][:, g, cols].bitcast(FP8X4),
+                    scales=act_scales[x][:, g, cols],
+                    in_=act_paired[(x, g)][:, half * K4 * HALF : (half + 1) * K4 * HALF],
+                )
+
+        def quantise_gate(name):
+            codes[name] = code_pool.tile([P, PASSES * PAIR], U32, name="codes", tag="codes", align_bytes=64)
+            scales[name] = code_pool.tile([P, PASSES * PAIR], U8, name="scales", tag="scales", align_bytes=64)
+            nc.vector.quantize_mx(out=codes[name][:].bitcast(FP8X4), scales=scales[name][:], in_=paired[name][:])
+
+        def quantise_proj(name, passes):
+            m, c = name[1], name[2]
+            cols = slice(c % 2 * PAIR, (c % 2 + 1) * PAIR)
+            for g in passes:
+                nc.vector.quantize_mx(
+                    out=proj_codes[:, m, g, c // 2, cols].bitcast(FP8X4),
+                    scales=proj_scales[:, m, g, c // 2, cols],
+                    in_=paired[name][:, g * K4 * PAIR : (g + 1) * K4 * PAIR],
+                )
+
+        def quantise(name):
+            if name[0] == WP:
+                quantise_proj(name, range(PASSES))
             else:
-                wc[nm] = wcp.tile([P, 512], U32, name="wc", tag="wc", align_bytes=64)
-                ws[nm] = wcp.tile([P, 512], U8, name="ws", tag="ws", align_bytes=64)
-                nc.vector.quantize_mx(out=wc[nm][:].bitcast(FP8X4), scales=ws[nm][:], in_=grp[nm][:])
+                quantise_gate(name)
 
-        acc = {}
+        spread = const.tile([P, VECTOR_COLUMNS], F32, name="spread")
+        bias_rz = const.tile([P, 2 * FT], F32, name="bias_rz")
 
-        def mx_group(key, j, q, xs, b):
-            bk = bank((key, j), [P, TOK], b)
-            n = 2 * len(xs)
-            i = 0
-            for x in xs:
-                a = ("agg", "mo")[x]
-                for g in range(2):
-                    cols = slice((2 * g + x) * P, (2 * g + x + 1) * P)
-                    nc.tensor.matmul_mx(
-                        out=bk[:],
-                        lhsT=wc[(q, j)][:, cols].bitcast(FP8X4),
-                        lhsT_scale=ws[(q, j)][:, cols],
-                        rhs=a_c[a][:, g, :].bitcast(FP8X4),
-                        rhs_scale=a_s[a][:, g, :],
-                        start=(i == 0),
-                        stop=(i == n - 1),
-                    )
-                    i += 1
-            acc[(key, j)] = bk
+        def spread_vectors():
+            out = bank("vectors", [P, SLOTS], BIAS_BANK)
+            nc.tensor.transpose(out[:, 0:P], vectors[:].bitcast(F32), ident[:])
+            spread_words = const.tile([P, VECTOR_COLUMNS // 2], F32, name="spread_words")
+            nc.vector.tensor_copy(out=spread_words[:], in_=out[:, 0 : VECTOR_COLUMNS // 2])
+            nc.vector.tensor_copy(out=spread[:], in_=spread_words[:].bitcast(BF16))
+            nc.vector.tensor_tensor(out=bias_rz[:], in0=spread[:, IH_R:IH_N], in1=spread[:, HH_R:HH_N], op=ALU.add)
 
-        bf = const.tile([P, 64], F32, name="bf")
-        brz = const.tile([P, 16], F32, name="brz")
+        def column(first, j):
+            return spread[:, first + j : first + j + 1]
 
-        def biases(b):
-            bk = bank("bias", [P, TOK], b)
-            nc.tensor.transpose(bk[:, 0:P], braw[:].bitcast(F32), ident[:])
-            bw = const.tile([P, 32], F32, name="bw")
-            nc.vector.tensor_copy(out=bw[:], in_=bk[:, 0:32])
-            nc.vector.tensor_copy(out=bf[:], in_=bw[:].bitcast(BF16))
-            nc.vector.tensor_tensor(out=brz[:], in0=bf[:, 0:16], in1=bf[:, 24:40], op=ALU.add)
+        sums = {}
+        gate = {}
 
-        tl = {}
+        def product(key, j, q, sources, number):
+            out = bank((key, j), [P, SLOTS], number)
+            steps = [(x, g) for x in sources for g in range(PASSES)]
+            for i, (x, g) in enumerate(steps):
+                cols = slice((2 * g + x) * P, (2 * g + x + 1) * P)
+                act = (AGG, MEM)[x]
+                nc.tensor.matmul_mx(
+                    out=out[:],
+                    lhsT=codes[(q, j)][:, cols].bitcast(FP8X4),
+                    lhsT_scale=scales[(q, j)][:, cols],
+                    rhs=act_codes[act][:, g, :].bitcast(FP8X4),
+                    rhs_scale=act_scales[act][:, g, :],
+                    start=(i == 0),
+                    stop=(i == len(steps) - 1),
+                )
+            sums[(key, j)] = out
 
-        def ew(j):
-            return nc.gpsimd if j < 7 else nc.vector
+        def gate_tile(key, j):
+            gate[(key, j)] = gate_pool.tile([P, SLOTS], F32, name="gate_" + key, tag="gate_" + key)
+            return gate[(key, j)]
 
-        def sig_r(j):
-            tl[("r", j)] = work.tile([P, TOK], F32, name="r", tag="r")
-            nc.scalar.activation(out=tl[("r", j)][:], in_=acc[("r", j)][:], func=ACT.Sigmoid, bias=brz[:, j : j + 1], scale=1.0)
+        def reset_gate(j):
+            nc.scalar.activation(out=gate_tile("r", j)[:], in_=sums[("r", j)][:], func=ACT.Sigmoid, bias=bias_rz[:, j : j + 1], scale=1.0)
 
-        def sig_z(j):
-            tl[("z", j)] = work.tile([P, TOK], F32, name="z", tag="z")
-            nc.scalar.activation(out=tl[("z", j)][:], in_=acc[("z", j)][:], func=ACT.Sigmoid, bias=brz[:, 8 + j : 9 + j], scale=1.0)
+        def update_gate(j, parts):
+            out = gate_tile("z", j)
+            for c in parts:
+                nc.scalar.activation(out=out[:, c], in_=sums[("z", j)][:, c], func=ACT.Sigmoid, bias=bias_rz[:, FT + j : FT + j + 1], scale=1.0)
 
-        def pre_n1(j):
-            t = work.tile([P, TOK], F32, name="t", tag="t")
-            tl[("t", j)] = t
-            nc.vector.scalar_tensor_tensor(out=t[:], in0=acc[("gh", j)][:], scalar=bf[:, 40 + j : 41 + j], in1=tl[("r", j)][:], op0=ALU.add, op1=ALU.mult)
+        def candidate_reset(j):
+            nc.vector.scalar_tensor_tensor(
+                out=gate_tile("c", j)[:], in0=sums[("gh", j)][:], scalar=column(HH_N, j), in1=gate[("r", j)][:], op0=ALU.add, op1=ALU.mult
+            )
 
-        def pre_n2(j):
-            t = tl[("t", j)]
-            nc.vector.tensor_tensor(out=t[:], in0=t[:], in1=acc[("gi", j)][:], op=ALU.add)
+        def candidate_sum(j):
+            c = gate[("c", j)]
+            nc.vector.tensor_tensor(out=c[:], in0=c[:], in1=sums[("gi", j)][:], op=ALU.add)
 
-        def tanh_n(j):
-            tl[("n", j)] = work.tile([P, TOK], F32, name="n", tag="n")
-            nc.scalar.activation(out=tl[("n", j)][:], in_=tl[("t", j)][:], func=ACT.Tanh, bias=bf[:, 16 + j : 17 + j], scale=1.0)
+        def candidate(j, parts):
+            out = gate_tile("n", j)
+            for c in parts:
+                nc.scalar.activation(out=out[:, c], in_=gate[("c", j)][:, c], func=ACT.Tanh, bias=column(IH_N, j), scale=1.0)
 
-        def blend_sub(j):
-            d = work.tile([P, TOK], F32, name="d", tag="d")
-            tl[("d", j)] = d
-            m = a_grp[("mo", j // 4)][:].rearrange("p (k t) -> p k t", t=4)[:, :, j % 4]
-            ew(j).tensor_tensor(out=d[:], in0=m, in1=tl[("n", j)][:], op=ALU.subtract)
+        def blend(j, engine, parts):
+            out = gate_tile("d", j)
+            old = act_paired[(MEM, j // K4)][:].rearrange("p (k t) -> p k t", t=K4)[:, :, j % K4]
+            n, z = gate[("n", j)], gate[("z", j)]
+            for c in parts:
+                engine.tensor_tensor(out=out[:, c], in0=old[:, c], in1=n[:, c], op=ALU.subtract)
+            for c in parts:
+                engine.tensor_tensor(out=out[:, c], in0=out[:, c], in1=z[:, c], op=ALU.mult)
+            for c in parts:
+                engine.tensor_tensor(out=hidden[:, j, c], in0=out[:, c], in1=n[:, c], op=ALU.add)
 
-        def blend_rest(j):
-            d = tl[("d", j)]
-            ew(j).tensor_tensor(out=d[:], in0=d[:], in1=tl[("z", j)][:], op=ALU.mult)
-            ew(j).tensor_tensor(out=hT[:, j, :], in0=d[:], in1=tl[("n", j)][:], op=ALU.add)
+        upright = {}
+        moments = {}
+        mean_var = {}
+        shifted = {}
+        inverse = {}
+        offset = {}
+        normal = {}
+        returned = {}
+        memory = {}
+        memory_paired = {}
+        projected = {}
 
-        hb = {}
-        mv = {}
-        ve = {}
-        rstd = {}
-        nmr = {}
-        xn = {}
-        bb = {}
-        mn = {}
-
-        def fwd(tt, half):
-            bk = bank(("F", tt, half), [P, TOK])
-            for jj in range(4):
-                nc.tensor.transpose(bk[:, jj * P : (jj + 1) * P], hT[:, 4 * half + jj, tt * P : (tt + 1) * P], ident[:])
-            hb[(tt, half)] = bk
-
-        def stats(tt, half):
-            if tt not in sts:
-                sts[tt] = lnp.tile([P, 2, 6], F32, name="st", tag="st")
-            nc.vector.bn_stats(out=sts[tt][:, half, :], in_=hb[(tt, half)][:])
-
-        sts = {}
-
-        def aggr(tt):
-            mv[tt] = lnp.tile([P, 2], F32, name="mv", tag="mv")
-            nc.vector.bn_aggr(out=mv[tt][:], in_=sts[tt][:].rearrange("p a b -> p (a b)"))
-
-        def eps(tt):
-            ve[tt] = lnp.tile([P, 1], F32, name="ve", tag="ve")
-            nc.vector.tensor_scalar(out=ve[tt][:], in0=mv[tt][:, 1:2], scalar1=EPS, scalar2=None, op0=ALU.add)
-
-        def root(tt):
-            rstd[tt] = lnp.tile([P, 1], F32, name="rstd", tag="rstd")
-            nc.gpsimd.tensor_tensor(out=rstd[tt][:], in0=ve[tt][:], in1=mhalf[:], op=ALU.pow)
-            nmr[tt] = lnp.tile([P, 1], F32, name="nmr", tag="nmr")
-            nc.gpsimd.tensor_scalar(out=nmr[tt][:], in0=mv[tt][:, 0:1], scalar1=rstd[tt][:, 0:1], scalar2=-1.0, op0=ALU.mult, op1=ALU.mult)
-
-        def norm(tt, engs):
-            xn[tt] = lnp.tile([P, D], F32, name="xn", tag="xn")
+        def turn_upright(s):
             for half in range(2):
-                dst = xn[tt][:, half * 512 : (half + 1) * 512]
-                if engs[half] == "S":
-                    nc.scalar.activation(out=dst, in_=hb[(tt, half)][:], func=ACT.Identity, bias=nmr[tt][:, 0:1], scale=rstd[tt][:, 0:1])
+                out = bank(("upright", s, half), [P, FT // 2 * P])
+                for i in range(FT // 2):
+                    nc.tensor.transpose(out[:, i * P : (i + 1) * P], hidden[:, FT // 2 * half + i, s * P : (s + 1) * P], ident[:])
+                upright[(s, half)] = out
+
+        def statistics(s, half):
+            if s not in moments:
+                moments[s] = ln_pool.tile([P, 2, 6], F32, name="moments", tag="moments")
+            nc.vector.bn_stats(out=moments[s][:, half, :], in_=upright[(s, half)][:])
+
+        def aggregate(s):
+            mean_var[s] = ln_pool.tile([P, 2], F32, name="mean_var", tag="mean_var")
+            nc.vector.bn_aggr(out=mean_var[s][:], in_=moments[s][:].rearrange("p a b -> p (a b)"))
+
+        def add_eps(s):
+            shifted[s] = ln_pool.tile([P, 1], F32, name="shifted", tag="shifted")
+            nc.vector.tensor_scalar(out=shifted[s][:], in0=mean_var[s][:, 1:2], scalar1=EPS, scalar2=None, op0=ALU.add)
+
+        def inverse_root(s):
+            inverse[s] = ln_pool.tile([P, 1], F32, name="inverse", tag="inverse")
+            nc.gpsimd.tensor_tensor(out=inverse[s][:], in0=shifted[s][:], in1=minus_half[:], op=ALU.pow)
+            offset[s] = ln_pool.tile([P, 1], F32, name="offset", tag="offset")
+            nc.gpsimd.tensor_scalar(
+                out=offset[s][:], in0=mean_var[s][:, 0:1], scalar1=inverse[s][:, 0:1], scalar2=-1.0, op0=ALU.mult, op1=ALU.mult
+            )
+
+        def normalise(s, engine):
+            normal[s] = ln_pool.tile([P, D], F32, name="normal", tag="normal")
+            for half in range(2):
+                dest = normal[s][:, half * D // 2 : (half + 1) * D // 2]
+                source = upright[(s, half)][:]
+                if engine == "S":
+                    nc.scalar.activation(out=dest, in_=source, func=ACT.Identity, bias=offset[s][:, 0:1], scale=inverse[s][:, 0:1])
                 else:
-                    nc.vector.tensor_scalar(out=dst, in0=hb[(tt, half)][:], scalar1=mv[tt][:, 0:1], scalar2=rstd[tt][:, 0:1], op0=ALU.subtract, op1=ALU.mult)
-                give(("F", tt, half))
-
-        def back(tt):
-            for g in range(2):
-                bk = bank(("B", tt, g), [P, 4, P])
-                for t in range(4):
-                    nc.tensor.transpose(bk[:, t, :], xn[tt][:, (4 * g + t) * P : (4 * g + t + 1) * P], ident[:])
-                bb[(tt, g)] = bk
-
-        def affine(tt, g, engs):
-            if g == 0:
-                mn[tt] = lnp.tile([P, 8, P], BF16, name="mn", tag="mn")
-            for t in range(4):
-                j = 4 * g + t
-                if engs[t] == "S":
-                    nc.scalar.activation(out=mn[tt][:, j, :], in_=bb[(tt, g)][:, t, :], func=ACT.Identity, bias=bf[:, 56 + j : 57 + j], scale=bf[:, 48 + j : 49 + j])
-                else:
-                    nc.vector.tensor_scalar(out=mn[tt][:, j, :], in0=bb[(tt, g)][:, t, :], scalar1=bf[:, 48 + j : 49 + j], scalar2=bf[:, 56 + j : 57 + j], op0=ALU.mult, op1=ALU.add)
-            give(("B", tt, g))
-
-        def regroup(tt, eng):
-            g2 = lnp.tile([P, 8 * P], BF16, name="g2", tag="g2", align_bytes=64)
-            for g in range(2):
-                dst = g2[:, g * 512 : (g + 1) * 512].rearrange("p (k t) -> p k t", t=4)
-                src = mn[tt][:, 4 * g : 4 * g + 4, :].rearrange("p t k -> p k t")
-                if eng == "V":
-                    nc.vector.tensor_copy(out=dst, in_=src)
-                else:
-                    nc.gpsimd.tensor_scalar(out=dst, in0=src, scalar1=1.0, scalar2=0.0, op0=ALU.mult, op1=ALU.add)
-            gq[tt] = g2
-
-        def quant2(tt):
-            nc.vector.quantize_mx(out=m2c[:, tt, :].bitcast(FP8X4), scales=m2s[:, tt, :], in_=gq[tt][:])
-
-        gq = {}
-        pb = {}
-
-        def project(tt, m, hs=(0, 1)):
-            for h in hs:
-                bk = bank(("P", tt, m, h), [P, TOK])
-                for g in range(2):
-                    nc.tensor.matmul_mx(
-                        out=bk[:],
-                        lhsT=m2c[:, tt, g * P : (g + 1) * P].bitcast(FP8X4),
-                        lhsT_scale=m2s[:, tt, g * P : (g + 1) * P],
-                        rhs=w2c[:, m, g, h, :].bitcast(FP8X4),
-                        rhs_scale=w2s[:, m, g, h, :],
-                        start=(g == 0),
-                        stop=(g == 1),
+                    nc.vector.tensor_scalar(
+                        out=dest, in0=source, scalar1=mean_var[s][:, 0:1], scalar2=inverse[s][:, 0:1], op0=ALU.subtract, op1=ALU.mult
                     )
-                pb[(tt, m, h)] = bk
+                release(("upright", s, half))
 
-        def results(tt, m, engs, hs=(0, 1)):
-            for h in hs:
-                osb = outp.tile([P, TOK], F32, name="osb", tag="osb")
-                copy_on(engs[h])(out=osb[:], in_=pb[(tt, m, h)][:])
-                give(("P", tt, m, h))
-                nc.sync.dma_start(out=outs[m][tt * P : (tt + 1) * P, h * TOK : (h + 1) * TOK], in_=osb[:])
+        def turn_back(s):
+            for g in range(PASSES):
+                out = bank(("back", s, g), [P, K4, P])
+                for t in range(K4):
+                    nc.tensor.transpose(out[:, t, :], normal[s][:, (K4 * g + t) * P : (K4 * g + t + 1) * P], ident[:])
+                returned[(s, g)] = out
 
-        def idle_work(n):
-            for i in range(n):
-                bk = bank("idle", [P, TOK], 6)
-                nc.tensor.matmul(out=bk[:], lhsT=zt[:, 0:P], rhs=zt[:], start=True, stop=True)
+        def gain_and_shift(s):
+            memory[s] = ln_pool.tile([P, FT, P], BF16, name="memory", tag="memory")
+            for g in range(PASSES):
+                for t in range(K4):
+                    j = K4 * g + t
+                    dest, source = memory[s][:, j, :], returned[(s, g)][:, t, :]
+                    if g == 0:
+                        nc.scalar.activation(out=dest, in_=source, func=ACT.Identity, bias=column(SHIFT, j), scale=column(GAIN, j))
+                    else:
+                        nc.vector.tensor_scalar(
+                            out=dest, in0=source, scalar1=column(GAIN, j), scalar2=column(SHIFT, j), op0=ALU.mult, op1=ALU.add
+                        )
+                release(("back", s, g))
 
-        tb = [0]
+        def pair_memory(s, engine):
+            memory_paired[s] = ln_pool.tile([P, D], BF16, name="memory_paired", tag="memory_paired", align_bytes=64)
+            for g in range(PASSES):
+                dest = memory_paired[s][:, g * K4 * P : (g + 1) * K4 * P].rearrange("p (k t) -> p k t", t=K4)
+                source = memory[s][:, K4 * g : K4 * g + K4, :].rearrange("p t k -> p k t")
+                if engine == "V":
+                    nc.vector.tensor_copy(out=dest, in_=source)
+                else:
+                    nc.gpsimd.tensor_scalar(out=dest, in0=source, scalar1=1.0, scalar2=0.0, op0=ALU.mult, op1=ALU.add)
 
-        def tr(nm):
-            transposes(nm, 2 * (tb[0] % 2))
-            tb[0] += 1
+        def quantise_memory(s):
+            nc.vector.quantize_mx(out=memory_codes[:, s, :].bitcast(FP8X4), scales=memory_scales[:, s, :], in_=memory_paired[s][:])
 
-        idle_work(WARM0)
-        for i, nm in enumerate(HEAD):
-            tr(nm)
-            idle_work(WH[i])
-            evacuate(nm, 0, HE[i][0])
-            evacuate(nm, 1, HE[i][1])
-            if nm[0] in ("agg", "mo"):
-                quantise_act(nm[0], 0, nm[1])
-                quantise_act(nm[0], 1, nm[1])
-            else:
-                quantise(nm)
-            if i == BI:
-                biases(7)
+        def project(s, m, h):
+            out = bank(("proj", s, m, h), [P, D // 2])
+            for g in range(PASSES):
+                nc.tensor.matmul_mx(
+                    out=out[:],
+                    lhsT=memory_codes[:, s, g * P : (g + 1) * P].bitcast(FP8X4),
+                    lhsT_scale=memory_scales[:, s, g * P : (g + 1) * P],
+                    rhs=proj_codes[:, m, g, h, :].bitcast(FP8X4),
+                    rhs_scale=proj_scales[:, m, g, h, :],
+                    start=(g == 0),
+                    stop=(g == PASSES - 1),
+                )
+            projected[(s, m, h)] = out
 
-        c3 = None
-        for j in range(8):
-            c1, c2 = stream[3 * j + 3], stream[3 * j + 4]
-            mx_group("r", j, 0, (0, 1), 4)
-            mx_group("gh", j, 2, (1,), 5)
+        def store(s, m, h, engine):
+            tile = out_pool.tile([P, D // 2], F32, name="out", tag="out")
+            copy_on(engine)(out=tile[:], in_=projected[(s, m, h)][:])
+            release(("proj", s, m, h))
+            nc.sync.dma_start(out=outs[m][s * P : (s + 1) * P, h * D // 2 : (h + 1) * D // 2], in_=tile[:])
+
+        def idle():
+            out = bank("idle", [P, SLOTS], IDLE_BANK)
+            nc.tensor.matmul(out=out[:], lhsT=zeros[:, 0:P], rhs=zeros[:], start=True, stop=True)
+
+        turn = [0]
+
+        def transpose_next(name):
+            transpose_load(name, 2 * (turn[0] % 2))
+            turn[0] += 1
+
+        for i in range(IDLE_FIRST):
+            idle()
+        for name in activations:
+            transpose_next(name)
+            idle()
+            copy_load(name, "SV")
+            quantise_activation(name)
+        for name in gate_chunks[0:2]:
+            transpose_next(name)
+            idle()
+            copy_load(name, "SS")
+            quantise(name)
+        spread_vectors()
+        transpose_next(gate_chunks[2])
+        copy_load(gate_chunks[2], "SV")
+        quantise(gate_chunks[2])
+
+        whole = (slice(0, SLOTS),)
+        halves = (slice(0, HALF), slice(HALF, SLOTS))
+        for j in range(FT):
+            first, second, third = chunks[3 * j + 3 : 3 * j + 6]
+            product("r", j, R, (0, 1), R_BANK)
+            product("gh", j, N, (1,), GH_BANK)
             if j > 0:
-                blend_sub(j - 1)
-                blend_rest(j - 1)
-                evacuate(c3, 0, "S")
-                evacuate(c3, 1, "V")
-            sig_r(j)
+                blend(j - 1, nc.gpsimd, whole)
+                copy_load(chunks[3 * j + 2], "SV")
+            reset_gate(j)
             if j > 0:
-                quantise(c3)
-            pre_n1(j)
-            tr(c1)
-            tr(c2)
-            evacuate(c1, 0, "S")
-            evacuate(c1, 1, "S")
-            evacuate(c2, 0, "S")
-            evacuate(c2, 1, "S")
-            mx_group("gi", j, 2, (0,), 6)
-            mx_group("z", j, 1, (0, 1), 7)
-            quantise(c1)
-            pre_n2(j)
-            if j < 7:
-                quantise(c2)
-                c3 = stream[3 * j + 5]
-                tr(c3)
-                tanh_n(j)
-                sig_z(j)
+                quantise(chunks[3 * j + 2])
+            candidate_reset(j)
+            transpose_next(first)
+            transpose_next(second)
+            copy_load(first, "SS")
+            copy_load(second, "SS")
+            product("gi", j, N, (0,), GI_BANK)
+            product("z", j, Z, (0, 1), Z_BANK)
+            quantise(first)
+            candidate_sum(j)
+            if j < LAST:
+                quantise(second)
+                transpose_next(third)
+                candidate(j, whole)
+                update_gate(j, whole)
 
-        w = stream[24:]
-        taken[0] = len(spare)
-        spare.extend([0, 1, 2, 3, 4, 5, 6])
-        halves = (slice(0, 256), slice(256, TOK))
-        for op in TAIL:
-            k = op[0]
-            if k == "tanh":
-                n = tl[("n", 7)] = work.tile([P, TOK], F32, name="n", tag="n")
-                for c in halves:
-                    nc.scalar.activation(out=n[:, c], in_=tl[("t", 7)][:, c], func=ACT.Tanh, bias=bf[:, 23:24], scale=1.0)
-            elif k == "sigz":
-                z = tl[("z", 7)] = work.tile([P, TOK], F32, name="g1", tag="g1")
-                for c in halves:
-                    nc.scalar.activation(out=z[:, c], in_=acc[("z", 7)][:, c], func=ACT.Sigmoid, bias=brz[:, 15:16], scale=1.0)
-                give(("z", 7))
-            elif k == "blend":
-                d = work.tile([P, TOK], F32, name="d", tag="d")
-                m = a_grp[("mo", 1)][:].rearrange("p (k t) -> p k t", t=4)[:, :, 3]
-                n, z = tl[("n", 7)], tl[("z", 7)]
-                for c in halves:
-                    nc.vector.tensor_tensor(out=d[:, c], in0=m[:, c], in1=n[:, c], op=ALU.subtract)
-                for c in halves:
-                    nc.vector.tensor_tensor(out=d[:, c], in0=d[:, c], in1=z[:, c], op=ALU.mult)
-                for c in halves:
-                    nc.vector.tensor_tensor(out=hT[:, 7, c], in0=d[:, c], in1=n[:, c], op=ALU.add)
-            elif k == "D":
-                bk = bank(("D", op[2]), [P, TOK])
-                for i in range(op[1]):
-                    nc.tensor.matmul(out=bk[:], lhsT=zt[:, 0:P], rhs=zt[:], start=True, stop=True)
-                give(("D", op[2]))
-            elif k == "T":
-                transposes(w[op[1]])
-            elif k == "E":
-                evacuate(w[op[1]], 0, op[2][0])
-                evacuate(w[op[1]], 1, op[2][1])
-            elif k == "Q":
-                quantise(w[op[1]], op[2:] or (0, 1))
-            elif k == "F":
-                for half in range(2):
-                    if (op[1], half) not in hb:
-                        fwd(op[1], half)
-            elif k == "f":
-                fwd(op[1], 0)
-            elif k == "s":
-                stats(op[1], 0)
-            elif k == "st":
-                if op[1] not in sts:
-                    stats(op[1], 0)
-                stats(op[1], 1)
-            elif k == "ag":
-                aggr(op[1])
-            elif k == "ve":
-                eps(op[1])
-            elif k == "sq":
-                root(op[1])
-            elif k == "nm":
-                norm(op[1], op[2])
-            elif k == "B":
-                back(op[1])
-            elif k == "af":
-                affine(op[1], 0, op[2][0] * 4)
-                affine(op[1], 1, op[2][1] * 4)
-            elif k == "rg":
-                regroup(op[1], op[2] if len(op) == 3 else "V")
-            elif k == "q2":
-                quant2(op[1])
-            elif k == "P":
-                project(op[1], op[2], op[3:] or (0, 1))
-            elif len(op) == 4:
-                results(op[1], op[2], op[3])
-            else:
-                results(op[1], op[2], op[4] * 2, (op[3],))
+        wp = proj_chunks
+        next_free[0] = len(free_banks)
+        free_banks.extend(range(Z_BANK))
+        transpose_load(wp[2])
+        transpose_load(wp[6])
+        candidate(LAST, halves)
+        update_gate(LAST, halves)
+        free_banks.extend([Z_BANK])
+        transpose_load(wp[7])
+        quantise(wp[1])
+        blend(LAST, nc.vector, halves)
+        copy_load(wp[2], "SS")
+        turn_upright(0)
+        turn_upright(1)
+        copy_load(wp[6], "SS")
+        transpose_load(wp[3])
+        copy_load(wp[7], "SS")
+        turn_upright(2)
+        copy_load(wp[3], "SS")
+        turn_upright(3)
+
+        def moments_of(s, name):
+            aggregate(s)
+            quantise_proj(name, (1,))
+            add_eps(s)
+            inverse_root(s)
+
+        for s, name in ((0, wp[2]), (1, wp[6])):
+            statistics(s, 0)
+            statistics(s, 1)
+            quantise_proj(name, (0,))
+            moments_of(s, name)
+        statistics(2, 0)
+        statistics(2, 1)
+        statistics(3, 0)
+        aggregate(2)
+        statistics(3, 1)
+        add_eps(2)
+        inverse_root(2)
+        quantise_proj(wp[3], (0,))
+        moments_of(3, wp[3])
+
+        normalise(0, "S")
+        turn_back(0)
+        normalise(1, "S")
+        turn_back(1)
+        gain_and_shift(0)
+        transpose_load(wp[5])
+        normalise(2, "S")
+        quantise_proj(wp[7], (0,))
+        pair_memory(0, "V")
+        quantise_proj(wp[7], (1,))
+        gain_and_shift(1)
+        turn_back(2)
+        copy_load(wp[5], "SS")
+        quantise_memory(0)
+        project(0, 0, 0)
+        project(0, 0, 1)
+        pair_memory(1, "V")
+        normalise(3, "V")
+        quantise_memory(1)
+        gain_and_shift(2)
+        turn_back(3)
+        project(0, 1, 1)
+        store(0, 0, 0, "S")
+        store(0, 0, 1, "S")
+        project(1, 0, 0)
+        project(1, 0, 1)
+        pair_memory(2, "G")
+        gain_and_shift(3)
+        pair_memory(3, "V")
+        quantise_memory(2)
+        transpose_load(wp[4])
+        store(0, 1, 1, "S")
+        project(1, 1, 1)
+        quantise(wp[5])
+        quantise_memory(3)
+        project(2, 0, 0)
+        project(2, 0, 1)
+        store(1, 0, 0, "S")
+        store(1, 0, 1, "V")
+        copy_load(wp[4], "SS")
+        project(2, 1, 1)
+        store(1, 1, 1, "S")
+        project(3, 0, 0)
+        project(3, 0, 1)
+        quantise(wp[4])
+        store(2, 0, 0, "S")
+        store(2, 0, 1, "V")
+
+        project(3, 1, 1)
+        project(0, 1, 0)
+        store(2, 1, 1, "S")
+        project(1, 1, 0)
+        store(3, 0, 0, "V")
+        store(3, 0, 1, "S")
+        project(2, 1, 0)
+        store(3, 1, 1, "V")
+        project(3, 1, 0)
+        for s in range(TILES):
+            store(s, 1, 0, "SV"[s % 2])

from contextlib import ExitStack

import concourse.masks as masks
import concourse.mybir as mybir

F32 = mybir.dt.float32
BF16 = mybir.dt.bfloat16
U32 = mybir.dt.uint32
I32 = mybir.dt.int32
U8 = mybir.dt.uint8
FP8X4 = mybir.dt.float8_e4m3fn_x4
ACT = mybir.ActivationFunctionType
ALU = mybir.AluOpType

P = 128
D = 1024
SLOTS = 512
TILES = SLOTS // P
HALF = SLOTS // 2
FT = D // P
LAST = FT - 1
K4 = 4
PASSES = D // (K4 * P)
PAIR = 2 * P
WORDS = 2 * PAIR
EPS = 1e-5

IH_R, IH_N = 0, 2 * FT
HH_R, HH_N = 3 * FT, 5 * FT
GAIN, SHIFT = 6 * FT, 7 * FT
VECTOR_COLUMNS = 8 * FT

R, Z, N = 0, 1, 2
AGG, MEM = "agg", "mem"
WP = "wp"

RAW_BUFS = 10
PAIRED_BUFS = 5
CODE_BUFS = 7
GATE_BUFS = 2
OUT_BUFS = 8
IDLE_FIRST = 4


def tile_instrumentspecificslotmemory_pb_kernel(
    tc, agg, M_old, W_ih, W_hh, b_ih, b_hh, g_mem, b_mem, Wk, Wv, out_0, out_1
):
    nc = tc.nc
    with ExitStack() as ctx:
        ctx.enter_context(tc.manual_schedule())
        const = ctx.enter_context(tc.tile_pool(name="const", bufs=1))
        raw_pool = ctx.enter_context(tc.tile_pool(name="raw", bufs=RAW_BUFS))
        paired_pool = ctx.enter_context(tc.tile_pool(name="paired", bufs=PAIRED_BUFS))
        code_pool = ctx.enter_context(tc.tile_pool(name="codes", bufs=CODE_BUFS))
        gate_pool = ctx.enter_context(tc.tile_pool(name="gates", bufs=GATE_BUFS))
        ln_pool = ctx.enter_context(tc.tile_pool(name="ln", bufs=TILES))
        out_pool = ctx.enter_context(tc.tile_pool(name="out", bufs=OUT_BUFS))
        psum = ctx.enter_context(tc.psum_pool(name="psum", bufs=1))

        BIAS_BANK, IDLE_BANK = 7, 6
        R_BANK, GH_BANK, GI_BANK, Z_BANK = 4, 5, 6, 7
        free_banks = []
        next_free = [0]
        owner = {}

        def bank(key, shape, number=None):
            if number is None:
                number = free_banks[next_free[0]]
                next_free[0] += 1
            owner[key] = number
            return psum.tile(shape, F32, name="b%d" % number, tag="b%d" % number)

        def release(key):
            free_banks.extend([owner[key]])

        act_rows = {
            AGG: agg.flatten_outer_dims().rearrange("(t p) k -> p t k", p=P),
            MEM: M_old.flatten_outer_dims().rearrange("(t p) k -> p t k", p=P),
        }
        gate_rows = [x.rearrange("(a p e) k -> p a e k", p=P, e=2) for x in (W_ih, W_hh)]
        proj_rows = [x.rearrange("(j p) k -> p j k", p=P) for x in (Wk, Wv)]
        outs = [out_0.flatten_outer_dims(), out_1.flatten_outer_dims()]

        activations = [(x, half) for x in (AGG, MEM) for half in range(2)]
        gate_chunks = [(q, j) for j in range(FT) for q in (R, N, Z)]
        proj_chunks = [(WP, m, c) for m in range(2) for c in range(D // PAIR)]
        chunks = gate_chunks + proj_chunks
        loads = activations + chunks
        raw = {}

        def load():
            if len(raw) < len(loads):
                name = loads[len(raw)]
                tile = raw_pool.tile([P, 2, D], BF16, name="raw", tag="raw")
                if name[0] == WP:
                    nc.sync.dma_start(out=tile[:], in_=proj_rows[name[1]][:, 2 * name[2] : 2 * name[2] + 2, :])
                elif name[0] in act_rows:
                    nc.sync.dma_start(out=tile[:], in_=act_rows[name[0]][:, 2 * name[1] : 2 * name[1] + 2, :])
                else:
                    q, j = name
                    for x in range(2):
                        nc.sync.dma_start(out=tile[:, x, :], in_=gate_rows[x][:, q * FT // 2 + j // 2, j % 2, :])
                raw[name] = tile

        ident = const.tile([P, P], F32, name="ident")
        masks.make_identity(nc, ident[:])
        vectors = const.tile([P, PAIR], BF16, name="vectors")
        nc.vector.memset(vectors[:].bitcast(I32), 0)
        row = 0
        for vector, length in ((b_ih, 3 * D), (b_hh, 3 * D), (g_mem, D), (b_mem, D)):
            rows = length // PAIR
            nc.scalar.dma_start(out=vectors[row : row + rows, :], in_=vector.rearrange("(a w) -> a w", w=PAIR))
            row += rows
        zeros = const.tile([P, SLOTS], BF16, name="zeros")
        nc.vector.memset(zeros[:].bitcast(I32), 0)
        for i in range(RAW_BUFS):
            load()
        minus_half = const.tile([P, 1], F32, name="minus_half")
        nc.vector.memset(minus_half[:], -0.5)
        table = const.tile([P, 1], F32, name="table")
        nc.scalar.activation(out=table[:], in_=minus_half[:], func=ACT.Sigmoid)

        act_paired = {
            (x, g): const.tile([P, K4 * SLOTS], BF16, name="paired_%s%d" % (x, g), align_bytes=64)
            for x in act_rows
            for g in range(PASSES)
        }
        act_codes = {x: const.tile([P, PASSES, SLOTS], U32, name="codes_" + x, align_bytes=64) for x in act_rows}
        act_scales = {x: const.tile([P, PASSES, SLOTS], U8, name="scales_" + x, align_bytes=64) for x in act_rows}
        proj_codes = const.tile([P, 2, PASSES, 2, D // 2], U32, name="proj_codes", align_bytes=64)
        proj_scales = const.tile([P, 2, PASSES, 2, D // 2], U8, name="proj_scales", align_bytes=64)
        hidden = const.tile([P, FT, SLOTS], F32, name="hidden")
        memory_codes = const.tile([P, TILES, PASSES * P], U32, name="memory_codes", align_bytes=64)
        memory_scales = const.tile([P, TILES, PASSES * P], U8, name="memory_scales", align_bytes=64)

        def copy_on(engine):
            return nc.scalar.copy if engine == "S" else nc.vector.tensor_copy

        turned = {}
        paired = {}
        codes = {}
        scales = {}

        def transpose_load(name, first_bank=None):
            words = raw[name][:].bitcast(F32)
            for g in range(PASSES):
                out = bank((name, g), [P, 2, PAIR], None if first_bank is None else first_bank + g)
                for u in range(2):
                    for s in range(2):
                        block = words[:, s, (2 * g + u) * P : (2 * g + u + 1) * P]
                        nc.tensor.transpose(out[:, u, s * P : (s + 1) * P], block, ident[:])
                turned[(name, g)] = out
            load()

        def copy_pass(name, g, engine):
            if name[0] in act_rows:
                dest = act_paired[(name[0], g)][:].bitcast(F32)[:, name[1] * WORDS : (name[1] + 1) * WORDS]
            else:
                if name not in paired:
                    paired[name] = paired_pool.tile([P, PASSES * K4 * PAIR], BF16, name="paired", tag="paired", align_bytes=64)
                dest = paired[name][:].bitcast(F32)[:, g * WORDS : (g + 1) * WORDS]
            source = turned[(name, g)][:].rearrange("p u o -> p o u")
            copy_on(engine)(out=dest.rearrange("p (o u) -> p o u", u=2), in_=source)
            release((name, g))

        def copy_load(name, engines):
            for g in range(PASSES):
                copy_pass(name, g, engines[g])

        def quantise_activation(name):
            x, half = name
            cols = slice(half * HALF, (half + 1) * HALF)
            for g in range(PASSES):
                nc.vector.quantize_mx(
                    out=act_codes[x][:, g, cols].bitcast(FP8X4),
                    scales=act_scales[x][:, g, cols],
                    in_=act_paired[(x, g)][:, half * K4 * HALF : (half + 1) * K4 * HALF],
                )

        def quantise_gate(name):
            codes[name] = code_pool.tile([P, PASSES * PAIR], U32, name="codes", tag="codes", align_bytes=64)
            scales[name] = code_pool.tile([P, PASSES * PAIR], U8, name="scales", tag="scales", align_bytes=64)
            nc.vector.quantize_mx(out=codes[name][:].bitcast(FP8X4), scales=scales[name][:], in_=paired[name][:])

        def quantise_proj(name, passes):
            m, c = name[1], name[2]
            cols = slice(c % 2 * PAIR, (c % 2 + 1) * PAIR)
            for g in passes:
                nc.vector.quantize_mx(
                    out=proj_codes[:, m, g, c // 2, cols].bitcast(FP8X4),
                    scales=proj_scales[:, m, g, c // 2, cols],
                    in_=paired[name][:, g * K4 * PAIR : (g + 1) * K4 * PAIR],
                )

        def quantise(name):
            if name[0] == WP:
                quantise_proj(name, range(PASSES))
            else:
                quantise_gate(name)

        spread = const.tile([P, VECTOR_COLUMNS], F32, name="spread")
        bias_rz = const.tile([P, 2 * FT], F32, name="bias_rz")

        def spread_vectors():
            out = bank("vectors", [P, SLOTS], BIAS_BANK)
            nc.tensor.transpose(out[:, 0:P], vectors[:].bitcast(F32), ident[:])
            spread_words = const.tile([P, VECTOR_COLUMNS // 2], F32, name="spread_words")
            nc.vector.tensor_copy(out=spread_words[:], in_=out[:, 0 : VECTOR_COLUMNS // 2])
            nc.vector.tensor_copy(out=spread[:], in_=spread_words[:].bitcast(BF16))
            nc.vector.tensor_tensor(out=bias_rz[:], in0=spread[:, IH_R:IH_N], in1=spread[:, HH_R:HH_N], op=ALU.add)

        def column(first, j):
            return spread[:, first + j : first + j + 1]

        sums = {}
        gate = {}

        def product(key, j, q, sources, number):
            out = bank((key, j), [P, SLOTS], number)
            steps = [(x, g) for x in sources for g in range(PASSES)]
            for i, (x, g) in enumerate(steps):
                cols = slice((2 * g + x) * P, (2 * g + x + 1) * P)
                act = (AGG, MEM)[x]
                nc.tensor.matmul_mx(
                    out=out[:],
                    lhsT=codes[(q, j)][:, cols].bitcast(FP8X4),
                    lhsT_scale=scales[(q, j)][:, cols],
                    rhs=act_codes[act][:, g, :].bitcast(FP8X4),
                    rhs_scale=act_scales[act][:, g, :],
                    start=(i == 0),
                    stop=(i == len(steps) - 1),
                )
            sums[(key, j)] = out

        def gate_tile(key, j):
            gate[(key, j)] = gate_pool.tile([P, SLOTS], F32, name="gate_" + key, tag="gate_" + key)
            return gate[(key, j)]

        def reset_gate(j):
            nc.scalar.activation(out=gate_tile("r", j)[:], in_=sums[("r", j)][:], func=ACT.Sigmoid, bias=bias_rz[:, j : j + 1], scale=1.0)

        def update_gate(j, parts):
            out = gate_tile("z", j)
            for c in parts:
                nc.scalar.activation(out=out[:, c], in_=sums[("z", j)][:, c], func=ACT.Sigmoid, bias=bias_rz[:, FT + j : FT + j + 1], scale=1.0)

        def candidate_reset(j):
            nc.vector.scalar_tensor_tensor(
                out=gate_tile("c", j)[:], in0=sums[("gh", j)][:], scalar=column(HH_N, j), in1=gate[("r", j)][:], op0=ALU.add, op1=ALU.mult
            )

        def candidate_sum(j):
            c = gate[("c", j)]
            nc.vector.tensor_tensor(out=c[:], in0=c[:], in1=sums[("gi", j)][:], op=ALU.add)

        def candidate(j, parts):
            out = gate_tile("n", j)
            for c in parts:
                nc.scalar.activation(out=out[:, c], in_=gate[("c", j)][:, c], func=ACT.Tanh, bias=column(IH_N, j), scale=1.0)

        def blend(j, engine, parts):
            out = gate_tile("d", j)
            old = act_paired[(MEM, j // K4)][:].rearrange("p (k t) -> p k t", t=K4)[:, :, j % K4]
            n, z = gate[("n", j)], gate[("z", j)]
            for c in parts:
                engine.tensor_tensor(out=out[:, c], in0=old[:, c], in1=n[:, c], op=ALU.subtract)
            for c in parts:
                engine.tensor_tensor(out=out[:, c], in0=out[:, c], in1=z[:, c], op=ALU.mult)
            for c in parts:
                engine.tensor_tensor(out=hidden[:, j, c], in0=out[:, c], in1=n[:, c], op=ALU.add)

        upright = {}
        moments = {}
        mean_var = {}
        shifted = {}
        inverse = {}
        offset = {}
        normal = {}
        returned = {}
        memory = {}
        memory_paired = {}
        projected = {}

        def turn_upright(s):
            for half in range(2):
                out = bank(("upright", s, half), [P, FT // 2 * P])
                for i in range(FT // 2):
                    nc.tensor.transpose(out[:, i * P : (i + 1) * P], hidden[:, FT // 2 * half + i, s * P : (s + 1) * P], ident[:])
                upright[(s, half)] = out

        def statistics(s, half):
            if s not in moments:
                moments[s] = ln_pool.tile([P, 2, 6], F32, name="moments", tag="moments")
            nc.vector.bn_stats(out=moments[s][:, half, :], in_=upright[(s, half)][:])

        def aggregate(s):
            mean_var[s] = ln_pool.tile([P, 2], F32, name="mean_var", tag="mean_var")
            nc.vector.bn_aggr(out=mean_var[s][:], in_=moments[s][:].rearrange("p a b -> p (a b)"))

        def add_eps(s):
            shifted[s] = ln_pool.tile([P, 1], F32, name="shifted", tag="shifted")
            nc.vector.tensor_scalar(out=shifted[s][:], in0=mean_var[s][:, 1:2], scalar1=EPS, scalar2=None, op0=ALU.add)

        def inverse_root(s):
            inverse[s] = ln_pool.tile([P, 1], F32, name="inverse", tag="inverse")
            nc.gpsimd.tensor_tensor(out=inverse[s][:], in0=shifted[s][:], in1=minus_half[:], op=ALU.pow)
            offset[s] = ln_pool.tile([P, 1], F32, name="offset", tag="offset")
            nc.gpsimd.tensor_scalar(
                out=offset[s][:], in0=mean_var[s][:, 0:1], scalar1=inverse[s][:, 0:1], scalar2=-1.0, op0=ALU.mult, op1=ALU.mult
            )

        def normalise(s, engine):
            normal[s] = ln_pool.tile([P, D], F32, name="normal", tag="normal")
            for half in range(2):
                dest = normal[s][:, half * D // 2 : (half + 1) * D // 2]
                source = upright[(s, half)][:]
                if engine == "S":
                    nc.scalar.activation(out=dest, in_=source, func=ACT.Identity, bias=offset[s][:, 0:1], scale=inverse[s][:, 0:1])
                else:
                    nc.vector.tensor_scalar(
                        out=dest, in0=source, scalar1=mean_var[s][:, 0:1], scalar2=inverse[s][:, 0:1], op0=ALU.subtract, op1=ALU.mult
                    )
                release(("upright", s, half))

        def turn_back(s):
            for g in range(PASSES):
                out = bank(("back", s, g), [P, K4, P])
                for t in range(K4):
                    nc.tensor.transpose(out[:, t, :], normal[s][:, (K4 * g + t) * P : (K4 * g + t + 1) * P], ident[:])
                returned[(s, g)] = out

        def gain_and_shift(s):
            memory[s] = ln_pool.tile([P, FT, P], BF16, name="memory", tag="memory")
            for g in range(PASSES):
                for t in range(K4):
                    j = K4 * g + t
                    dest, source = memory[s][:, j, :], returned[(s, g)][:, t, :]
                    if g == 0:
                        nc.scalar.activation(out=dest, in_=source, func=ACT.Identity, bias=column(SHIFT, j), scale=column(GAIN, j))
                    else:
                        nc.vector.tensor_scalar(
                            out=dest, in0=source, scalar1=column(GAIN, j), scalar2=column(SHIFT, j), op0=ALU.mult, op1=ALU.add
                        )
                release(("back", s, g))

        def pair_memory(s, engine):
            memory_paired[s] = ln_pool.tile([P, D], BF16, name="memory_paired", tag="memory_paired", align_bytes=64)
            for g in range(PASSES):
                dest = memory_paired[s][:, g * K4 * P : (g + 1) * K4 * P].rearrange("p (k t) -> p k t", t=K4)
                source = memory[s][:, K4 * g : K4 * g + K4, :].rearrange("p t k -> p k t")
                if engine == "V":
                    nc.vector.tensor_copy(out=dest, in_=source)
                else:
                    nc.gpsimd.tensor_scalar(out=dest, in0=source, scalar1=1.0, scalar2=0.0, op0=ALU.mult, op1=ALU.add)

        def quantise_memory(s):
            nc.vector.quantize_mx(out=memory_codes[:, s, :].bitcast(FP8X4), scales=memory_scales[:, s, :], in_=memory_paired[s][:])

        def project(s, m, h):
            out = bank(("proj", s, m, h), [P, D // 2])
            for g in range(PASSES):
                nc.tensor.matmul_mx(
                    out=out[:],
                    lhsT=memory_codes[:, s, g * P : (g + 1) * P].bitcast(FP8X4),
                    lhsT_scale=memory_scales[:, s, g * P : (g + 1) * P],
                    rhs=proj_codes[:, m, g, h, :].bitcast(FP8X4),
                    rhs_scale=proj_scales[:, m, g, h, :],
                    start=(g == 0),
                    stop=(g == PASSES - 1),
                )
            projected[(s, m, h)] = out

        def store(s, m, h, engine):
            tile = out_pool.tile([P, D // 2], F32, name="out", tag="out")
            copy_on(engine)(out=tile[:], in_=projected[(s, m, h)][:])
            release(("proj", s, m, h))
            nc.sync.dma_start(out=outs[m][s * P : (s + 1) * P, h * D // 2 : (h + 1) * D // 2], in_=tile[:])

        def idle():
            out = bank("idle", [P, SLOTS], IDLE_BANK)
            nc.tensor.matmul(out=out[:], lhsT=zeros[:, 0:P], rhs=zeros[:], start=True, stop=True)

        turn = [0]

        def transpose_next(name):
            transpose_load(name, 2 * (turn[0] % 2))
            turn[0] += 1

        for i in range(IDLE_FIRST):
            idle()
        for name in activations:
            transpose_next(name)
            idle()
            copy_load(name, "SV")
            quantise_activation(name)
        for name in gate_chunks[0:2]:
            transpose_next(name)
            idle()
            copy_load(name, "SS")
            quantise(name)
        spread_vectors()
        transpose_next(gate_chunks[2])
        copy_load(gate_chunks[2], "SV")
        quantise(gate_chunks[2])

        whole = (slice(0, SLOTS),)
        halves = (slice(0, HALF), slice(HALF, SLOTS))
        for j in range(FT):
            first, second, third = chunks[3 * j + 3 : 3 * j + 6]
            product("r", j, R, (0, 1), R_BANK)
            product("gh", j, N, (1,), GH_BANK)
            if j > 0:
                blend(j - 1, nc.gpsimd, whole)
                copy_load(chunks[3 * j + 2], "SV")
            reset_gate(j)
            if j > 0:
                quantise(chunks[3 * j + 2])
            candidate_reset(j)
            transpose_next(first)
            transpose_next(second)
            copy_load(first, "SS")
            copy_load(second, "SS")
            product("gi", j, N, (0,), GI_BANK)
            product("z", j, Z, (0, 1), Z_BANK)
            quantise(first)
            candidate_sum(j)
            if j < LAST:
                quantise(second)
                transpose_next(third)
                candidate(j, whole)
                update_gate(j, whole)

        wp = proj_chunks
        next_free[0] = len(free_banks)
        free_banks.extend(range(Z_BANK))
        transpose_load(wp[2])
        transpose_load(wp[6])
        candidate(LAST, halves)
        update_gate(LAST, halves)
        free_banks.extend([Z_BANK])
        transpose_load(wp[7])
        quantise(wp[1])
        blend(LAST, nc.vector, halves)
        copy_load(wp[2], "SS")
        turn_upright(0)
        turn_upright(1)
        copy_load(wp[6], "SS")
        transpose_load(wp[3])
        copy_load(wp[7], "SS")
        turn_upright(2)
        copy_load(wp[3], "SS")
        turn_upright(3)

        def moments_of(s, name):
            aggregate(s)
            quantise_proj(name, (1,))
            add_eps(s)
            inverse_root(s)

        for s, name in ((0, wp[2]), (1, wp[6])):
            statistics(s, 0)
            statistics(s, 1)
            quantise_proj(name, (0,))
            moments_of(s, name)
        statistics(2, 0)
        statistics(2, 1)
        statistics(3, 0)
        aggregate(2)
        statistics(3, 1)
        add_eps(2)
        inverse_root(2)
        quantise_proj(wp[3], (0,))
        moments_of(3, wp[3])

        normalise(0, "S")
        turn_back(0)
        normalise(1, "S")
        turn_back(1)
        gain_and_shift(0)
        transpose_load(wp[5])
        normalise(2, "S")
        quantise_proj(wp[7], (0,))
        pair_memory(0, "V")
        quantise_proj(wp[7], (1,))
        gain_and_shift(1)
        turn_back(2)
        copy_load(wp[5], "SS")
        quantise_memory(0)
        project(0, 0, 0)
        project(0, 0, 1)
        pair_memory(1, "V")
        normalise(3, "V")
        quantise_memory(1)
        gain_and_shift(2)
        turn_back(3)
        project(0, 1, 1)
        store(0, 0, 0, "S")
        store(0, 0, 1, "S")
        project(1, 0, 0)
        project(1, 0, 1)
        pair_memory(2, "G")
        gain_and_shift(3)
        pair_memory(3, "V")
        quantise_memory(2)
        transpose_load(wp[4])
        store(0, 1, 1, "S")
        project(1, 1, 1)
        quantise(wp[5])
        quantise_memory(3)
        project(2, 0, 0)
        project(2, 0, 1)
        store(1, 0, 0, "S")
        store(1, 0, 1, "V")
        copy_load(wp[4], "SS")
        project(2, 1, 1)
        store(1, 1, 1, "S")
        project(3, 0, 0)
        project(3, 0, 1)
        quantise(wp[4])
        store(2, 0, 0, "S")
        store(2, 0, 1, "V")

        project(3, 1, 1)
        project(0, 1, 0)
        store(2, 1, 1, "S")
        project(1, 1, 0)
        store(3, 0, 0, "V")
        store(3, 0, 1, "S")
        project(2, 1, 0)
        store(3, 1, 1, "V")
        project(3, 1, 0)
        for s in range(TILES):
            store(s, 1, 0, "SV"[s % 2])
